import numpy as np
import ml_dtypes


def mxq(x, axis, fmt="e4m3"):
    dtype, down = {"e4m3": (ml_dtypes.float8_e4m3fn, 7), "e5m2": (ml_dtypes.float8_e5m2, 14)}[fmt]
    v = np.moveaxis(np.asarray(x, np.float32).astype(ml_dtypes.bfloat16).astype(np.float64), axis, -1)
    blocks = v.reshape(v.shape[:-1] + (-1, 32))
    amax = np.abs(blocks).max(-1, keepdims=True)
    byte = np.maximum(np.where(amax > 0, np.frexp(amax)[1] - 1 + 127, 0) - down, 1)
    scale = np.exp2(byte - 127.0)
    codes = (blocks / scale).astype(np.float32).astype(dtype).astype(np.float64)
    return np.moveaxis((codes * scale).reshape(v.shape), -1, axis)


WIDE = False


def mx_kscale(k):
    if not WIDE:
        return np.ones(k)
    levels = np.array([10, -10, 5, -5, 0])
    a = np.random.permutation(np.resize(levels, k // 512 * 4)).reshape(k // 512, 4)
    idx = np.arange(k)
    return np.exp2(a[idx // 512, idx % 128 // 32])


BF16 = ml_dtypes.bfloat16


def bf(x):
    return np.asarray(x, np.float32).astype(BF16)


def f64(x):
    return np.asarray(x).astype(np.float64)


E2M1 = np.array([0.0, 0.5, 1.0, 1.5, 2.0, 3.0, 4.0, 6.0, -0.0, -0.5, -1.0, -1.5, -2.0, -3.0, -4.0, -6.0])


def pack_weight(w, fmt):
    k, n = w.shape
    w = f64(bf(w)).reshape(k // 32, 32, n)
    amax = np.abs(w).max(1)
    if fmt == "e4m3":
        byte = np.frexp(amax)[1] - 1 + 127 - 7
    else:
        mant, ex = np.frexp(amax / 6.0)
        byte = np.where(mant > 0.5, ex, ex - 1) + 127
    byte = np.clip(np.where(amax > 0, byte, 1), 1, 254)
    scaled = (w * np.exp2(127.0 - byte)[:, None, :]).reshape(k, n).astype(np.float32)
    by_word = np.ascontiguousarray(scaled.reshape(k // 512, 128, 4, n).transpose(0, 1, 3, 2))
    if fmt == "e4m3":
        words = by_word.astype(ml_dtypes.float8_e4m3fn).view(np.uint8)
    else:
        c = by_word.astype(ml_dtypes.float4_e2m1fn).view(np.uint8) & 0xF
        words = c[..., 0::2] | (c[..., 1::2] << 4)
    return np.ascontiguousarray(words), np.ascontiguousarray(byte.astype(np.uint8).reshape(k // 512, 16, n))


def unpack_weight(words, scales, fmt):
    g, p, n, _ = words.shape
    if fmt == "e4m3":
        vals = np.ascontiguousarray(words).view(ml_dtypes.float8_e4m3fn).astype(np.float64)
    else:
        nib = np.empty((g, p, n, 4), np.uint8)
        nib[..., 0::2] = words & 0xF
        nib[..., 1::2] = words >> 4
        vals = E2M1[nib]
    vals = vals * np.repeat(np.exp2(scales.astype(np.float64) - 127.0), 8, axis=1)[..., None]
    return vals.transpose(0, 1, 3, 2).reshape(g * 512, n)

def pack4(w):
    words, scales = pack_weight(w, "e2m1")
    return words.reshape(words.shape[0], 128, -1), scales


def unpack4(words, scales):
    return unpack_weight(words.reshape(words.shape[0], 128, -1, 2), scales, "e2m1")


B, T, C, N_HEAD, N_KV, HD, WINDOW = 1, 1024, 1024, 8, 2, 128, 512
QPK = N_HEAD // N_KV
TOT = QPK + 2
QKV_OUT = N_KV * TOT * HD


def apply_rope(xh, fc):
    b, t, h, d = xh.shape
    xs = xh.reshape(b, t, h, d // 2, 2)
    f = fc.reshape(1, t, 1, d // 2, 2)
    re = xs[..., 0] * f[..., 0] - xs[..., 1] * f[..., 1]
    im = xs[..., 1] * f[..., 0] + xs[..., 0] * f[..., 1]
    return np.stack([re, im], axis=-1).reshape(b, t, h, d)


def setup_inputs():
    s = mx_kscale(C)
    inv_freq = 1.0 / (10000.0 ** (np.arange(0, HD, 2) / HD))
    ang = np.outer(np.arange(T), inv_freq)
    x = bf(np.random.standard_normal((B, T, C)) * s)
    freqs_cis = bf(np.stack([np.cos(ang), np.sin(ang)], axis=-1))
    words, scales = pack4(np.random.standard_normal((C, QKV_OUT)) * 1.5 / np.sqrt(C) / s[:, None])
    return {"x": x,
            "freqs_cis": freqs_cis,
            "W_attn_words": words,
            "W_attn_scales": scales}


def reference(x, freqs_cis, W_attn_words, W_attn_scales):
    qkv = mxq(f64(x), 2, "e4m3") @ unpack4(W_attn_words, W_attn_scales)
    qkv = qkv.reshape(B, T, N_KV, TOT, HD).transpose(0, 2, 3, 1, 4)
    q = qkv[:, :, :QPK].reshape(B, -1, N_HEAD, HD)
    k = qkv[:, :, QPK:QPK + 1].reshape(B, -1, N_KV, HD)
    v = qkv[:, :, QPK + 1:].reshape(B, -1, N_KV, HD)
    fc = f64(freqs_cis)
    return apply_rope(q, fc), apply_rope(k, fc), v

@@ -1,0 +1,227 @@
+from contextlib import ExitStack
+
+import concourse.mybir as mybir
+from concourse.masks import make_identity
+
+F32 = mybir.dt.float32
+BF16 = mybir.dt.bfloat16
+I32 = mybir.dt.int32
+U32 = mybir.dt.uint32
+U8 = mybir.dt.uint8
+FP8X4 = mybir.dt.float8_e4m3fn_x4
+FP4X4 = mybir.dt.float4_e2m1fn_x4
+MULT = mybir.AluOpType.mult
+ADD = mybir.AluOpType.add
+
+P = 128
+TOKENS = 1024
+K = 1024
+HD = 128
+PAIRS = HD // 2
+GROUPS = 2
+Q_SLOTS = 4
+GROUP_COLS = (Q_SLOTS + 2) * HD
+COLS = GROUPS * GROUP_COLS
+K_PASS = 4 * P
+PASSES = K // K_PASS
+TILES = TOKENS // P
+BANK = 512
+Q_BANKS = GROUPS * Q_SLOTS * HD // BANK
+BLOCKS = BANK // HD
+TILES_PER_STORE = 2
+AHEAD = 2
+
+FLOPS = 2 * TOKENS * K * COLS
+
+
+def tile_causalselfattentiongqa_pa_kernel(
+    tc, x, freqs_cis, W_attn_words, W_attn_scales, out_0, out_1, out_2
+):
+    nc = tc.nc
+    with ExitStack() as ctx:
+        keep = ctx.enter_context(tc.tile_pool(name="keep", bufs=1))
+        stage = ctx.enter_context(tc.tile_pool(name="stage", bufs=2))
+        products = ctx.enter_context(tc.tile_pool(name="products", bufs=3))
+        results = ctx.enter_context(tc.tile_pool(name="results", bufs=2))
+        flipped = ctx.enter_context(tc.psum_pool(name="flipped", bufs=2))
+        sums = ctx.enter_context(tc.psum_pool(name="sums", bufs=6))
+
+        x_view = x.rearrange("o (p r) k -> (o p) r k", r=TILES)
+        q_rows = out_0.rearrange("o n h f -> (o n h) f").rearrange(
+            "(s p r) f -> p s r f", p=P, r=TILES
+        )
+        k_rows = out_1.rearrange("o n h f -> (o n h) f").rearrange(
+            "(g p r) f -> p g r f", p=P, r=TILES
+        )
+        v_rows = out_2.rearrange("o n h f -> (o n h) f").rearrange(
+            "(g p r) f -> p g r f", p=P, r=TILES
+        )
+        words_i32 = W_attn_words.bitcast(I32)
+        scales_i32 = W_attn_scales.bitcast(I32)
+
+        x_sb = keep.tile([P, TILES, K], BF16)
+        x_codes = keep.tile([P, TILES, PASSES * P], U32, align_bytes=64)
+        x_scales = keep.tile([P, TILES, PASSES * P], U8, align_bytes=64)
+        w_words = keep.tile([P, PASSES, 2 * COLS], U8, align_bytes=64)
+        w_scales = keep.tile([P, PASSES, COLS], U8, align_bytes=64)
+        w_scales_raw = keep.tile([P, PASSES, COLS], U8, align_bytes=64)
+        cd_q = keep.tile([P, GROUPS * Q_SLOTS, HD], BF16)
+        dc_q = keep.tile([P, GROUPS * Q_SLOTS, HD], BF16)
+        cd_k = keep.tile([P, GROUPS, TILES // 2, HD], BF16)
+        dc_k = keep.tile([P, GROUPS, TILES // 2, HD], BF16)
+        identity = keep.tile([P, P], F32)
+
+        nc.vector.memset(w_scales_raw[:].bitcast(I32), 0)
+        make_identity(nc, identity[:])
+        for quadrant in range(4):
+            nc.sync.dma_start(
+                out=w_scales_raw[32 * quadrant : 32 * quadrant + 4, :, :].bitcast(I32),
+                in_=scales_i32[:, 4 * quadrant : 4 * quadrant + 4, :].rearrange("g r n -> r g n"),
+            )
+
+        def load_x(first_tile):
+            tiles = slice(first_tile, first_tile + TILES_PER_STORE)
+            nc.sync.dma_start(out=x_sb[:, tiles, :], in_=x_view[:, tiles, :])
+
+        def load_words(first_byte, block_bytes, hbm_first_byte):
+            for c in range(PASSES):
+                nc.sync.dma_start(
+                    out=w_words[:, c, first_byte : first_byte + GROUPS * block_bytes]
+                    .bitcast(I32)
+                    .rearrange("p (g n) -> p g n", g=GROUPS),
+                    in_=words_i32[c].rearrange("p (g n) -> p g n", g=GROUPS)[
+                        :, :, hbm_first_byte // 4 : (hbm_first_byte + block_bytes) // 4
+                    ],
+                )
+
+        q_bytes = 2 * Q_SLOTS * HD
+        kv_bytes = 2 * 2 * HD
+        load_x(0)
+        load_words(0, q_bytes, 0)
+        nc.sync.dma_start(out=cd_q[:], in_=freqs_cis.rearrange("(s p) i c -> p s (i c)", p=P))
+        nc.sync.dma_start(
+            out=cd_k[:].rearrange("p g j f -> p g (j f)"),
+            in_=freqs_cis.rearrange("(g p j) i c -> p g (j i c)", g=GROUPS, p=P),
+        )
+        load_x(TILES_PER_STORE)
+        load_words(GROUPS * q_bytes, kv_bytes, q_bytes)
+        for first_tile in range(2 * TILES_PER_STORE, TILES, TILES_PER_STORE):
+            load_x(first_tile)
+
+        raw = w_scales_raw[:].bitcast(I32).rearrange("p c (g n) -> p c g n", g=GROUPS)
+        q_words = Q_SLOTS * HD // 4
+        nc.vector.tensor_copy(
+            out=w_scales[:, :, 0 : GROUPS * Q_SLOTS * HD]
+            .bitcast(I32)
+            .rearrange("p c (g n) -> p c g n", g=GROUPS),
+            in_=raw[:, :, :, 0:q_words],
+        )
+        nc.vector.tensor_copy(
+            out=w_scales[:, :, GROUPS * Q_SLOTS * HD : COLS]
+            .bitcast(I32)
+            .rearrange("p c (g n) -> p c g n", g=GROUPS),
+            in_=raw[:, :, :, q_words : GROUP_COLS // 4],
+        )
+
+        def turned_table(dc, cd):
+            cd_pairs = cd.rearrange("p (n two) -> p n two", two=2)
+            dc_pairs = dc.rearrange("p (n two) -> p n two", two=2)
+            nc.gpsimd.tensor_scalar(
+                out=dc_pairs[:, :, 0:1], in0=cd_pairs[:, :, 1:2], scalar1=-1.0, scalar2=0.0, op0=MULT, op1=ADD
+            )
+            nc.gpsimd.tensor_scalar(
+                out=dc_pairs[:, :, 1:2], in0=cd_pairs[:, :, 0:1], scalar1=1.0, scalar2=0.0, op0=MULT, op1=ADD
+            )
+
+        turned_table(dc_q[:].rearrange("p s f -> p (s f)"), cd_q[:].rearrange("p s f -> p (s f)"))
+        turned_table(dc_k[:].rearrange("p g j f -> p (g j f)"), cd_k[:].rearrange("p g j f -> p (g j f)"))
+
+        def quantise_tile(r):
+            x_words = x_sb[:, r, :].bitcast(F32)
+            turned = flipped.tile([P, PASSES, 2, P], F32)
+            for c in range(PASSES):
+                for u in range(2):
+                    nc.tensor.transpose(
+                        turned[:, c, u, :],
+                        x_words[:, K_PASS // 2 * c + u : K_PASS // 2 * (c + 1) : 2],
+                        identity[:],
+                    )
+            grouped = stage.tile([P, PASSES * P * 4], BF16, align_bytes=64)
+            nc.scalar.copy(
+                out=grouped[:].bitcast(F32).rearrange("p (c t u) -> p c t u", c=PASSES, u=2),
+                in_=turned[:].rearrange("p c u t -> p c t u"),
+            )
+            nc.vector.quantize_mx(
+                out=x_codes[:, r, :].bitcast(FP8X4), scales=x_scales[:, r, :], in_=grouped[:]
+            )
+
+        def project(r, bank):
+            acc = sums.tile([P, BANK], F32)
+            for c in range(PASSES):
+                nc.tensor.matmul_mx(
+                    out=acc[:],
+                    lhsT=x_codes[:, r, P * c : P * (c + 1)].bitcast(FP8X4),
+                    lhsT_scale=x_scales[:, r, P * c : P * (c + 1)],
+                    rhs=w_words[:, c, 2 * BANK * bank : 2 * BANK * (bank + 1)].bitcast(FP4X4),
+                    rhs_scale=w_scales[:, c, BANK * bank : BANK * (bank + 1)],
+                    start=(c == 0),
+                    stop=(c == PASSES - 1),
+                )
+            return acc
+
+        def rotate(dst, u, cd, dc):
+            shape = [P, u.shape[1], PAIRS, 2]
+            nc.vector.tensor_tensor(out=dst, in0=u[:, :, :, 0:1].to_broadcast(shape), in1=cd, op=MULT)
+            b_part = products.tile(shape, F32)
+            nc.vector.tensor_tensor(out=b_part[:], in0=u[:, :, :, 1:2].to_broadcast(shape), in1=dc, op=MULT)
+            nc.gpsimd.tensor_tensor(out=dst, in0=dst, in1=b_part[:], op=ADD)
+
+        def by_pairs(blocks):
+            return blocks.rearrange("p s (i two) -> p s i two", two=2)
+
+        def multiply_and_rotate(r, out_tiles):
+            place = r % TILES_PER_STORE
+            for bank in range(Q_BANKS):
+                acc = project(r, bank)
+                blocks = slice(BLOCKS * bank, BLOCKS * (bank + 1))
+                rotate(
+                    by_pairs(out_tiles["q%d" % bank][:, :, place, :]),
+                    by_pairs(acc[:].rearrange("p (s f) -> p s f", f=HD)),
+                    by_pairs(cd_q[:, blocks, :]),
+                    by_pairs(dc_q[:, blocks, :]),
+                )
+            acc = project(r, Q_BANKS)
+            kv = acc[:].rearrange("p (g two f) -> p g two f", two=2, f=HD)
+            rotate(
+                by_pairs(out_tiles["k"][:, :, place, :]),
+                by_pairs(kv[:, :, 0, :]),
+                by_pairs(cd_k[:, :, r // 2, :]),
+                by_pairs(dc_k[:, :, r // 2, :]),
+            )
+            nc.scalar.copy(out=out_tiles["v"][:, :, place, :], in_=kv[:, :, 1, :])
+
+        def store(first_tile, out_tiles):
+            tiles = slice(first_tile, first_tile + TILES_PER_STORE)
+            for bank in range(Q_BANKS):
+                nc.sync.dma_start(
+                    out=q_rows[:, BLOCKS * bank : BLOCKS * (bank + 1), tiles, :], in_=out_tiles["q%d" % bank][:]
+                )
+            nc.sync.dma_start(out=k_rows[:, :, tiles, :], in_=out_tiles["k"][:])
+            nc.sync.dma_start(out=v_rows[:, :, tiles, :], in_=out_tiles["v"][:])
+
+        for r in range(AHEAD):
+            quantise_tile(r)
+        out_tiles = {}
+        for r in range(TILES):
+            if r % TILES_PER_STORE == 0:
+                out_tiles = {
+                    "q0": results.tile([P, BLOCKS, TILES_PER_STORE, HD], F32, name="q0"),
+                    "q1": results.tile([P, BLOCKS, TILES_PER_STORE, HD], F32, name="q1"),
+                    "k": results.tile([P, GROUPS, TILES_PER_STORE, HD], F32, name="k"),
+                    "v": results.tile([P, GROUPS, TILES_PER_STORE, HD], F32, name="v"),
+                }
+            multiply_and_rotate(r, out_tiles)
+            if r + AHEAD < TILES:
+                quantise_tile(r + AHEAD)
+            if r % TILES_PER_STORE == TILES_PER_STORE - 1:
+                store(r + 1 - TILES_PER_STORE, out_tiles)

@@ -28,8 +28,7 @@ TILES = TOKENS // P
 BANK = 512
 Q_BANKS = GROUPS * Q_SLOTS * HD // BANK
 BLOCKS = BANK // HD
-TILES_PER_STORE = 2
-AHEAD = 2
+PAIR = 2
 
 FLOPS = 2 * TOKENS * K * COLS
 
@@ -40,9 +39,9 @@ def tile_causalselfattentiongqa_pa_kernel(
     nc = tc.nc
     with ExitStack() as ctx:
         keep = ctx.enter_context(tc.tile_pool(name="keep", bufs=1))
-        stage = ctx.enter_context(tc.tile_pool(name="stage", bufs=2))
-        products = ctx.enter_context(tc.tile_pool(name="products", bufs=3))
-        results = ctx.enter_context(tc.tile_pool(name="results", bufs=2))
+        stage = ctx.enter_context(tc.tile_pool(name="stage", bufs=3))
+        products = ctx.enter_context(tc.tile_pool(name="products", bufs=4))
+        results = ctx.enter_context(tc.tile_pool(name="results", bufs=4))
         flipped = ctx.enter_context(tc.psum_pool(name="flipped", bufs=2))
         sums = ctx.enter_context(tc.psum_pool(name="sums", bufs=6))
 
@@ -56,7 +55,7 @@ def tile_causalselfattentiongqa_pa_kernel(
         v_rows = out_2.rearrange("o n h f -> (o n h) f").rearrange(
             "(g p r) f -> p g r f", p=P, r=TILES
         )
-        words_i32 = W_attn_words.bitcast(I32)
+        words_i32 = W_attn_words.bitcast(I32).rearrange("c p n -> p c n")
         scales_i32 = W_attn_scales.bitcast(I32)
 
         x_sb = keep.tile([P, TILES, K], BF16)
@@ -73,40 +72,42 @@ def tile_causalselfattentiongqa_pa_kernel(
 
         nc.vector.memset(w_scales_raw[:].bitcast(I32), 0)
         make_identity(nc, identity[:])
+
+        def load_x(first_tile, count):
+            tiles = slice(first_tile, first_tile + count)
+            nc.sync.dma_start(out=x_sb[:, tiles, :], in_=x_view[:, tiles, :])
+
+        def load_words(first_byte, hbm_first_byte, n_bytes):
+            nc.sync.dma_start(
+                out=w_words[:, :, first_byte : first_byte + n_bytes].bitcast(I32),
+                in_=words_i32[:, :, hbm_first_byte // 4 : (hbm_first_byte + n_bytes) // 4],
+            )
+
+        q_bytes = 2 * Q_SLOTS * HD
+        kv_bytes = 2 * 2 * HD
+        group_bytes = q_bytes + kv_bytes
+        fc_q = freqs_cis.rearrange("(s p) i c -> p s (i c)", p=P)
+
+        load_x(0, 1)
+        load_words(0, 0, q_bytes)
         for quadrant in range(4):
             nc.sync.dma_start(
                 out=w_scales_raw[32 * quadrant : 32 * quadrant + 4, :, :].bitcast(I32),
                 in_=scales_i32[:, 4 * quadrant : 4 * quadrant + 4, :].rearrange("g r n -> r g n"),
             )
-
-        def load_x(first_tile):
-            tiles = slice(first_tile, first_tile + TILES_PER_STORE)
-            nc.sync.dma_start(out=x_sb[:, tiles, :], in_=x_view[:, tiles, :])
-
-        def load_words(first_byte, block_bytes, hbm_first_byte):
-            for c in range(PASSES):
-                nc.sync.dma_start(
-                    out=w_words[:, c, first_byte : first_byte + GROUPS * block_bytes]
-                    .bitcast(I32)
-                    .rearrange("p (g n) -> p g n", g=GROUPS),
-                    in_=words_i32[c].rearrange("p (g n) -> p g n", g=GROUPS)[
-                        :, :, hbm_first_byte // 4 : (hbm_first_byte + block_bytes) // 4
-                    ],
-                )
-
-        q_bytes = 2 * Q_SLOTS * HD
-        kv_bytes = 2 * 2 * HD
-        load_x(0)
-        load_words(0, q_bytes, 0)
-        nc.sync.dma_start(out=cd_q[:], in_=freqs_cis.rearrange("(s p) i c -> p s (i c)", p=P))
+        nc.sync.dma_start(out=cd_q[:, 0:BLOCKS, :], in_=fc_q[:, 0:BLOCKS, :])
+        load_x(1, 1)
+        load_x(2, 2)
+        load_x(4, 2)
+        load_x(6, 2)
+        load_words(q_bytes, group_bytes, q_bytes)
+        nc.sync.dma_start(out=cd_q[:, BLOCKS : 2 * BLOCKS, :], in_=fc_q[:, BLOCKS : 2 * BLOCKS, :])
+        for g in range(GROUPS):
+            load_words(GROUPS * q_bytes + g * kv_bytes, g * group_bytes + q_bytes, kv_bytes)
         nc.sync.dma_start(
             out=cd_k[:].rearrange("p g j f -> p g (j f)"),
             in_=freqs_cis.rearrange("(g p j) i c -> p g (j i c)", g=GROUPS, p=P),
         )
-        load_x(TILES_PER_STORE)
-        load_words(GROUPS * q_bytes, kv_bytes, q_bytes)
-        for first_tile in range(2 * TILES_PER_STORE, TILES, TILES_PER_STORE):
-            load_x(first_tile)
 
         raw = w_scales_raw[:].bitcast(I32).rearrange("p c (g n) -> p c g n", g=GROUPS)
         q_words = Q_SLOTS * HD // 4
@@ -133,30 +134,38 @@ def tile_causalselfattentiongqa_pa_kernel(
                 out=dc_pairs[:, :, 1:2], in0=cd_pairs[:, :, 0:1], scalar1=1.0, scalar2=0.0, op0=MULT, op1=ADD
             )
 
-        turned_table(dc_q[:].rearrange("p s f -> p (s f)"), cd_q[:].rearrange("p s f -> p (s f)"))
+        for bank in range(Q_BANKS):
+            blocks = slice(BLOCKS * bank, BLOCKS * (bank + 1))
+            turned_table(
+                dc_q[:, blocks, :].rearrange("p s f -> p (s f)"), cd_q[:, blocks, :].rearrange("p s f -> p (s f)")
+            )
         turned_table(dc_k[:].rearrange("p g j f -> p (g j f)"), cd_k[:].rearrange("p g j f -> p (g j f)"))
 
-        def quantise_tile(r):
-            x_words = x_sb[:, r, :].bitcast(F32)
-            turned = flipped.tile([P, PASSES, 2, P], F32)
-            for c in range(PASSES):
-                for u in range(2):
-                    nc.tensor.transpose(
-                        turned[:, c, u, :],
-                        x_words[:, K_PASS // 2 * c + u : K_PASS // 2 * (c + 1) : 2],
-                        identity[:],
-                    )
-            grouped = stage.tile([P, PASSES * P * 4], BF16, align_bytes=64)
-            nc.scalar.copy(
-                out=grouped[:].bitcast(F32).rearrange("p (c t u) -> p c t u", c=PASSES, u=2),
-                in_=turned[:].rearrange("p c u t -> p c t u"),
-            )
+        def quantise_tiles(first_tile, count):
+            grouped = stage.tile([P, count, PASSES * P * 4], BF16, align_bytes=64, name="grouped")
+            for n in range(count):
+                x_words = x_sb[:, first_tile + n, :].bitcast(F32)
+                turned = flipped.tile([P, PASSES, 2, P], F32, name="turned")
+                for c in range(PASSES):
+                    for u in range(2):
+                        nc.tensor.transpose(
+                            turned[:, c, u, :],
+                            x_words[:, K_PASS // 2 * c + u : K_PASS // 2 * (c + 1) : 2],
+                            identity[:],
+                        )
+                nc.scalar.copy(
+                    out=grouped[:, n, :].bitcast(F32).rearrange("p (c t u) -> p c t u", c=PASSES, u=2),
+                    in_=turned[:].rearrange("p c u t -> p c t u"),
+                )
+            tiles = slice(first_tile, first_tile + count)
             nc.vector.quantize_mx(
-                out=x_codes[:, r, :].bitcast(FP8X4), scales=x_scales[:, r, :], in_=grouped[:]
+                out=x_codes[:, tiles, :].rearrange("p r w -> p (r w)").bitcast(FP8X4),
+                scales=x_scales[:, tiles, :].rearrange("p r w -> p (r w)"),
+                in_=grouped[:].rearrange("p r w -> p (r w)"),
             )
 
         def project(r, bank):
-            acc = sums.tile([P, BANK], F32)
+            acc = sums.tile([P, BANK], F32, name="acc")
             for c in range(PASSES):
                 nc.tensor.matmul_mx(
                     out=acc[:],
@@ -169,59 +178,63 @@ def tile_causalselfattentiongqa_pa_kernel(
                 )
             return acc
 
-        def rotate(dst, u, cd, dc):
-            shape = [P, u.shape[1], PAIRS, 2]
-            nc.vector.tensor_tensor(out=dst, in0=u[:, :, :, 0:1].to_broadcast(shape), in1=cd, op=MULT)
-            b_part = products.tile(shape, F32)
-            nc.vector.tensor_tensor(out=b_part[:], in0=u[:, :, :, 1:2].to_broadcast(shape), in1=dc, op=MULT)
-            nc.gpsimd.tensor_tensor(out=dst, in0=dst, in1=b_part[:], op=ADD)
-
         def by_pairs(blocks):
             return blocks.rearrange("p s (i two) -> p s i two", two=2)
 
-        def multiply_and_rotate(r, out_tiles):
-            place = r % TILES_PER_STORE
-            for bank in range(Q_BANKS):
-                acc = project(r, bank)
-                blocks = slice(BLOCKS * bank, BLOCKS * (bank + 1))
-                rotate(
-                    by_pairs(out_tiles["q%d" % bank][:, :, place, :]),
+        def two_products(a_part, b_part, u, cd, dc):
+            shape = [P, u.shape[1], PAIRS, 2]
+            nc.vector.tensor_tensor(out=a_part, in0=u[:, :, :, 0:1].to_broadcast(shape), in1=cd, op=MULT)
+            nc.vector.tensor_tensor(out=b_part, in0=u[:, :, :, 1:2].to_broadcast(shape), in1=dc, op=MULT)
+
+        def add_up(a_part, b_part):
+            flat_a = a_part[:].rearrange("p s t f -> p (s t f)")
+            nc.gpsimd.tensor_tensor(out=flat_a, in0=flat_a, in1=b_part[:].rearrange("p s t f -> p (s t f)"), op=ADD)
+
+        def queries(bank, pair):
+            blocks = slice(BLOCKS * bank, BLOCKS * (bank + 1))
+            a_part = results.tile([P, BLOCKS, PAIR, HD], F32, name="q_a")
+            b_part = products.tile([P, BLOCKS, PAIR, HD], F32, name="q_b")
+            for place in range(PAIR):
+                acc = project(PAIR * pair + place, bank)
+                two_products(
+                    by_pairs(a_part[:, :, place, :]),
+                    by_pairs(b_part[:, :, place, :]),
                     by_pairs(acc[:].rearrange("p (s f) -> p s f", f=HD)),
                     by_pairs(cd_q[:, blocks, :]),
                     by_pairs(dc_q[:, blocks, :]),
                 )
-            acc = project(r, Q_BANKS)
-            kv = acc[:].rearrange("p (g two f) -> p g two f", two=2, f=HD)
-            rotate(
-                by_pairs(out_tiles["k"][:, :, place, :]),
-                by_pairs(kv[:, :, 0, :]),
-                by_pairs(cd_k[:, :, r // 2, :]),
-                by_pairs(dc_k[:, :, r // 2, :]),
-            )
-            nc.scalar.copy(out=out_tiles["v"][:, :, place, :], in_=kv[:, :, 1, :])
+            add_up(a_part, b_part)
+            nc.sync.dma_start(out=q_rows[:, blocks, PAIR * pair : PAIR * (pair + 1), :], in_=a_part[:])
 
-        def store(first_tile, out_tiles):
-            tiles = slice(first_tile, first_tile + TILES_PER_STORE)
-            for bank in range(Q_BANKS):
-                nc.sync.dma_start(
-                    out=q_rows[:, BLOCKS * bank : BLOCKS * (bank + 1), tiles, :], in_=out_tiles["q%d" % bank][:]
+        def keys_and_values(pair):
+            a_part = results.tile([P, GROUPS, PAIR, HD], F32, name="k_a")
+            b_part = products.tile([P, GROUPS, PAIR, HD], F32, name="k_b")
+            values = results.tile([P, GROUPS, PAIR, HD], F32, name="v")
+            for place in range(PAIR):
+                acc = project(PAIR * pair + place, Q_BANKS)
+                kv = acc[:].rearrange("p (g two f) -> p g two f", two=2, f=HD)
+                two_products(
+                    by_pairs(a_part[:, :, place, :]),
+                    by_pairs(b_part[:, :, place, :]),
+                    by_pairs(kv[:, :, 0, :]),
+                    by_pairs(cd_k[:, :, pair, :]),
+                    by_pairs(dc_k[:, :, pair, :]),
                 )
-            nc.sync.dma_start(out=k_rows[:, :, tiles, :], in_=out_tiles["k"][:])
-            nc.sync.dma_start(out=v_rows[:, :, tiles, :], in_=out_tiles["v"][:])
+                nc.scalar.copy(out=values[:, :, place, :], in_=kv[:, :, 1, :])
+            tiles = slice(PAIR * pair, PAIR * (pair + 1))
+            nc.sync.dma_start(out=v_rows[:, :, tiles, :], in_=values[:])
+            add_up(a_part, b_part)
+            nc.sync.dma_start(out=k_rows[:, :, tiles, :], in_=a_part[:])
 
-        for r in range(AHEAD):
-            quantise_tile(r)
-        out_tiles = {}
-        for r in range(TILES):
-            if r % TILES_PER_STORE == 0:
-                out_tiles = {
-                    "q0": results.tile([P, BLOCKS, TILES_PER_STORE, HD], F32, name="q0"),
-                    "q1": results.tile([P, BLOCKS, TILES_PER_STORE, HD], F32, name="q1"),
-                    "k": results.tile([P, GROUPS, TILES_PER_STORE, HD], F32, name="k"),
-                    "v": results.tile([P, GROUPS, TILES_PER_STORE, HD], F32, name="v"),
-                }
-            multiply_and_rotate(r, out_tiles)
-            if r + AHEAD < TILES:
-                quantise_tile(r + AHEAD)
-            if r % TILES_PER_STORE == TILES_PER_STORE - 1:
-                store(r + 1 - TILES_PER_STORE, out_tiles)
+        pairs = TILES // PAIR
+        quantise_tiles(0, 1)
+        quantise_tiles(1, 1)
+        quantise_tiles(2, 2)
+        for pair in range(pairs):
+            queries(0, pair)
+            if pair + 2 < pairs:
+                quantise_tiles(PAIR * (pair + 2), PAIR)
+        for pair in range(pairs):
+            queries(1, pair)
+        for pair in range(pairs):
+            keys_and_values(pair)

@@ -63,65 +63,43 @@ def tile_causalselfattentiongqa_pa_kernel(
         x_scales = keep.tile([P, TILES, PASSES * P], U8, align_bytes=64)
         w_words = keep.tile([P, PASSES, 2 * COLS], U8, align_bytes=64)
         w_scales = keep.tile([P, PASSES, COLS], U8, align_bytes=64)
-        w_scales_raw = keep.tile([P, PASSES, COLS], U8, align_bytes=64)
         cd_q = keep.tile([P, GROUPS * Q_SLOTS, HD], BF16)
         dc_q = keep.tile([P, GROUPS * Q_SLOTS, HD], BF16)
         cd_k = keep.tile([P, GROUPS, TILES // 2, HD], BF16)
         dc_k = keep.tile([P, GROUPS, TILES // 2, HD], BF16)
         identity = keep.tile([P, P], F32)
 
-        nc.vector.memset(w_scales_raw[:].bitcast(I32), 0)
+        nc.vector.memset(w_scales[:].bitcast(I32), 0)
         make_identity(nc, identity[:])
 
         def load_x(first_tile, count):
             tiles = slice(first_tile, first_tile + count)
             nc.sync.dma_start(out=x_sb[:, tiles, :], in_=x_view[:, tiles, :])
 
-        def load_words(first_byte, hbm_first_byte, n_bytes):
+        def load_words(first_byte, n_bytes):
             nc.sync.dma_start(
                 out=w_words[:, :, first_byte : first_byte + n_bytes].bitcast(I32),
-                in_=words_i32[:, :, hbm_first_byte // 4 : (hbm_first_byte + n_bytes) // 4],
+                in_=words_i32[:, :, first_byte // 4 : (first_byte + n_bytes) // 4],
             )
 
         q_bytes = 2 * Q_SLOTS * HD
-        kv_bytes = 2 * 2 * HD
-        group_bytes = q_bytes + kv_bytes
         fc_q = freqs_cis.rearrange("(s p) i c -> p s (i c)", p=P)
 
         load_x(0, 1)
-        load_words(0, 0, q_bytes)
+        load_words(0, q_bytes)
         for quadrant in range(4):
             nc.sync.dma_start(
-                out=w_scales_raw[32 * quadrant : 32 * quadrant + 4, :, :].bitcast(I32),
+                out=w_scales[32 * quadrant : 32 * quadrant + 4, :, :].bitcast(I32),
                 in_=scales_i32[:, 4 * quadrant : 4 * quadrant + 4, :].rearrange("g r n -> r g n"),
             )
-        nc.sync.dma_start(out=cd_q[:, 0:BLOCKS, :], in_=fc_q[:, 0:BLOCKS, :])
+        nc.sync.dma_start(out=cd_q[:], in_=fc_q)
         load_x(1, 1)
         load_x(2, 2)
-        load_x(4, 2)
-        load_x(6, 2)
-        load_words(q_bytes, group_bytes, q_bytes)
-        nc.sync.dma_start(out=cd_q[:, BLOCKS : 2 * BLOCKS, :], in_=fc_q[:, BLOCKS : 2 * BLOCKS, :])
-        for g in range(GROUPS):
-            load_words(GROUPS * q_bytes + g * kv_bytes, g * group_bytes + q_bytes, kv_bytes)
+        load_x(4, 4)
+        load_words(q_bytes, 2 * COLS - q_bytes)
         nc.sync.dma_start(
             out=cd_k[:].rearrange("p g j f -> p g (j f)"),
             in_=freqs_cis.rearrange("(g p j) i c -> p g (j i c)", g=GROUPS, p=P),
-        )
-
-        raw = w_scales_raw[:].bitcast(I32).rearrange("p c (g n) -> p c g n", g=GROUPS)
-        q_words = Q_SLOTS * HD // 4
-        nc.vector.tensor_copy(
-            out=w_scales[:, :, 0 : GROUPS * Q_SLOTS * HD]
-            .bitcast(I32)
-            .rearrange("p c (g n) -> p c g n", g=GROUPS),
-            in_=raw[:, :, :, 0:q_words],
-        )
-        nc.vector.tensor_copy(
-            out=w_scales[:, :, GROUPS * Q_SLOTS * HD : COLS]
-            .bitcast(I32)
-            .rearrange("p c (g n) -> p c g n", g=GROUPS),
-            in_=raw[:, :, :, q_words : GROUP_COLS // 4],
         )
 
         def turned_table(dc, cd):
@@ -134,12 +112,17 @@ def tile_causalselfattentiongqa_pa_kernel(
                 out=dc_pairs[:, :, 1:2], in0=cd_pairs[:, :, 0:1], scalar1=1.0, scalar2=0.0, op0=MULT, op1=ADD
             )
 
+        def turned_table_on_scalar(dc, cd):
+            cd_pairs = cd.rearrange("p (n two) -> p n two", two=2)
+            dc_pairs = dc.rearrange("p (n two) -> p n two", two=2)
+            nc.scalar.mul(out=dc_pairs[:, :, 0:1], in_=cd_pairs[:, :, 1:2], mul=-1.0)
+            nc.scalar.copy(out=dc_pairs[:, :, 1:2], in_=cd_pairs[:, :, 0:1])
+
         for bank in range(Q_BANKS):
             blocks = slice(BLOCKS * bank, BLOCKS * (bank + 1))
             turned_table(
                 dc_q[:, blocks, :].rearrange("p s f -> p (s f)"), cd_q[:, blocks, :].rearrange("p s f -> p (s f)")
             )
-        turned_table(dc_k[:].rearrange("p g j f -> p (g j f)"), cd_k[:].rearrange("p g j f -> p (g j f)"))
 
         def quantise_tiles(first_tile, count):
             grouped = stage.tile([P, count, PASSES * P * 4], BF16, align_bytes=64, name="grouped")
@@ -164,18 +147,31 @@ def tile_causalselfattentiongqa_pa_kernel(
                 in_=grouped[:].rearrange("p r w -> p (r w)"),
             )
 
-        def project(r, bank):
-            acc = sums.tile([P, BANK], F32, name="acc")
+        def multiply(acc, r, first_col, n_cols):
             for c in range(PASSES):
                 nc.tensor.matmul_mx(
-                    out=acc[:],
+                    out=acc,
                     lhsT=x_codes[:, r, P * c : P * (c + 1)].bitcast(FP8X4),
                     lhsT_scale=x_scales[:, r, P * c : P * (c + 1)],
-                    rhs=w_words[:, c, 2 * BANK * bank : 2 * BANK * (bank + 1)].bitcast(FP4X4),
-                    rhs_scale=w_scales[:, c, BANK * bank : BANK * (bank + 1)],
+                    rhs=w_words[:, c, 2 * first_col : 2 * (first_col + n_cols)].bitcast(FP4X4),
+                    rhs_scale=w_scales[:, c, first_col : first_col + n_cols],
                     start=(c == 0),
                     stop=(c == PASSES - 1),
                 )
+
+        def project(r, bank):
+            acc = sums.tile([P, BANK], F32, name="acc")
+            if bank < Q_BANKS:
+                multiply(acc[:], r, GROUP_COLS * bank, BANK)
+            else:
+                for g in range(GROUPS):
+                    for slot in range(2):
+                        multiply(
+                            acc[:, HD * (2 * g + slot) : HD * (2 * g + slot + 1)],
+                            r,
+                            GROUP_COLS * g + HD * (Q_SLOTS + slot),
+                            HD,
+                        )
             return acc
 
         def by_pairs(blocks):
@@ -186,11 +182,11 @@ def tile_causalselfattentiongqa_pa_kernel(
             nc.vector.tensor_tensor(out=a_part, in0=u[:, :, :, 0:1].to_broadcast(shape), in1=cd, op=MULT)
             nc.vector.tensor_tensor(out=b_part, in0=u[:, :, :, 1:2].to_broadcast(shape), in1=dc, op=MULT)
 
-        def add_up(a_part, b_part):
+        def add_up(a_part, b_part, engine):
             flat_a = a_part[:].rearrange("p s t f -> p (s t f)")
-            nc.gpsimd.tensor_tensor(out=flat_a, in0=flat_a, in1=b_part[:].rearrange("p s t f -> p (s t f)"), op=ADD)
+            engine.tensor_tensor(out=flat_a, in0=flat_a, in1=b_part[:].rearrange("p s t f -> p (s t f)"), op=ADD)
 
-        def queries(bank, pair):
+        def queries(bank, pair, engine):
             blocks = slice(BLOCKS * bank, BLOCKS * (bank + 1))
             a_part = results.tile([P, BLOCKS, PAIR, HD], F32, name="q_a")
             b_part = products.tile([P, BLOCKS, PAIR, HD], F32, name="q_b")
@@ -203,27 +199,30 @@ def tile_causalselfattentiongqa_pa_kernel(
                     by_pairs(cd_q[:, blocks, :]),
                     by_pairs(dc_q[:, blocks, :]),
                 )
-            add_up(a_part, b_part)
+            add_up(a_part, b_part, engine)
             nc.sync.dma_start(out=q_rows[:, blocks, PAIR * pair : PAIR * (pair + 1), :], in_=a_part[:])
 
-        def keys_and_values(pair):
-            a_part = results.tile([P, GROUPS, PAIR, HD], F32, name="k_a")
-            b_part = products.tile([P, GROUPS, PAIR, HD], F32, name="k_b")
-            values = results.tile([P, GROUPS, PAIR, HD], F32, name="v")
-            for place in range(PAIR):
-                acc = project(PAIR * pair + place, Q_BANKS)
+        QUAD = 4
+
+        def keys_and_values(quad):
+            a_part = results.tile([P, GROUPS, QUAD, HD], F32, name="k_a")
+            b_part = products.tile([P, GROUPS, QUAD, HD], F32, name="k_b")
+            values = results.tile([P, GROUPS, QUAD, HD], F32, name="v")
+            for place in range(QUAD):
+                r = QUAD * quad + place
+                acc = project(r, Q_BANKS)
                 kv = acc[:].rearrange("p (g two f) -> p g two f", two=2, f=HD)
                 two_products(
                     by_pairs(a_part[:, :, place, :]),
                     by_pairs(b_part[:, :, place, :]),
                     by_pairs(kv[:, :, 0, :]),
-                    by_pairs(cd_k[:, :, pair, :]),
-                    by_pairs(dc_k[:, :, pair, :]),
+                    by_pairs(cd_k[:, :, r // 2, :]),
+                    by_pairs(dc_k[:, :, r // 2, :]),
                 )
                 nc.scalar.copy(out=values[:, :, place, :], in_=kv[:, :, 1, :])
-            tiles = slice(PAIR * pair, PAIR * (pair + 1))
+            tiles = slice(QUAD * quad, QUAD * (quad + 1))
             nc.sync.dma_start(out=v_rows[:, :, tiles, :], in_=values[:])
-            add_up(a_part, b_part)
+            add_up(a_part, b_part, nc.gpsimd)
             nc.sync.dma_start(out=k_rows[:, :, tiles, :], in_=a_part[:])
 
         pairs = TILES // PAIR
@@ -231,10 +230,11 @@ def tile_causalselfattentiongqa_pa_kernel(
         quantise_tiles(1, 1)
         quantise_tiles(2, 2)
         for pair in range(pairs):
-            queries(0, pair)
+            queries(0, pair, nc.gpsimd)
             if pair + 2 < pairs:
                 quantise_tiles(PAIR * (pair + 2), PAIR)
+        turned_table_on_scalar(dc_k[:].rearrange("p g j f -> p (g j f)"), cd_k[:].rearrange("p g j f -> p (g j f)"))
+        for quad in range(TILES // QUAD):
+            keys_and_values(quad)
         for pair in range(pairs):
-            queries(1, pair)
-        for pair in range(pairs):
-            keys_and_values(pair)
+            queries(1, pair, nc.vector if pair == pairs - 1 else nc.gpsimd)

@@ -40,7 +40,6 @@ def tile_causalselfattentiongqa_pa_kernel(
     with ExitStack() as ctx:
         keep = ctx.enter_context(tc.tile_pool(name="keep", bufs=1))
         stage = ctx.enter_context(tc.tile_pool(name="stage", bufs=3))
-        products = ctx.enter_context(tc.tile_pool(name="products", bufs=4))
         results = ctx.enter_context(tc.tile_pool(name="results", bufs=4))
         flipped = ctx.enter_context(tc.psum_pool(name="flipped", bufs=2))
         sums = ctx.enter_context(tc.psum_pool(name="sums", bufs=6))
@@ -63,10 +62,8 @@ def tile_causalselfattentiongqa_pa_kernel(
         x_scales = keep.tile([P, TILES, PASSES * P], U8, align_bytes=64)
         w_words = keep.tile([P, PASSES, 2 * COLS], U8, align_bytes=64)
         w_scales = keep.tile([P, PASSES, COLS], U8, align_bytes=64)
-        cd_q = keep.tile([P, GROUPS * Q_SLOTS, HD], BF16)
-        dc_q = keep.tile([P, GROUPS * Q_SLOTS, HD], BF16)
-        cd_k = keep.tile([P, GROUPS, TILES // 2, HD], BF16)
-        dc_k = keep.tile([P, GROUPS, TILES // 2, HD], BF16)
+        table_q = keep.tile([P, 2, GROUPS * Q_SLOTS, HD], BF16)
+        table_k = keep.tile([P, 2, GROUPS, TILES // 2, HD], BF16)
         identity = keep.tile([P, P], F32)
 
         nc.vector.memset(w_scales[:].bitcast(I32), 0)
@@ -92,13 +89,13 @@ def tile_causalselfattentiongqa_pa_kernel(
                 out=w_scales[32 * quadrant : 32 * quadrant + 4, :, :].bitcast(I32),
                 in_=scales_i32[:, 4 * quadrant : 4 * quadrant + 4, :].rearrange("g r n -> r g n"),
             )
-        nc.sync.dma_start(out=cd_q[:], in_=fc_q)
+        nc.sync.dma_start(out=table_q[:, 0, :, :], in_=fc_q)
         load_x(1, 1)
         load_x(2, 2)
         load_x(4, 4)
         load_words(q_bytes, 2 * COLS - q_bytes)
         nc.sync.dma_start(
-            out=cd_k[:].rearrange("p g j f -> p g (j f)"),
+            out=table_k[:, 0, :, :, :].rearrange("p g j f -> p g (j f)"),
             in_=freqs_cis.rearrange("(g p j) i c -> p g (j i c)", g=GROUPS, p=P),
         )
 
@@ -121,7 +118,8 @@ def tile_causalselfattentiongqa_pa_kernel(
         for bank in range(Q_BANKS):
             blocks = slice(BLOCKS * bank, BLOCKS * (bank + 1))
             turned_table(
-                dc_q[:, blocks, :].rearrange("p s f -> p (s f)"), cd_q[:, blocks, :].rearrange("p s f -> p (s f)")
+                table_q[:, 1, blocks, :].rearrange("p s f -> p (s f)"),
+                table_q[:, 0, blocks, :].rearrange("p s f -> p (s f)"),
             )
 
         def quantise_tiles(first_tile, count):
@@ -167,63 +165,55 @@ def tile_causalselfattentiongqa_pa_kernel(
                 for g in range(GROUPS):
                     for slot in range(2):
                         multiply(
-                            acc[:, HD * (2 * g + slot) : HD * (2 * g + slot + 1)],
+                            acc[:, HD * (GROUPS * slot + g) : HD * (GROUPS * slot + g + 1)],
                             r,
                             GROUP_COLS * g + HD * (Q_SLOTS + slot),
                             HD,
                         )
             return acc
 
-        def by_pairs(blocks):
-            return blocks.rearrange("p s (i two) -> p s i two", two=2)
+        def both_products(parts, u, table):
+            n_blocks = parts.shape[2]
+            nc.vector.tensor_tensor(
+                out=parts.rearrange("p w s (i two) -> p w s i two", two=2),
+                in0=u.rearrange("p (s i w) -> p w s i", i=PAIRS, w=2)
+                .unsqueeze(4)
+                .to_broadcast([P, 2, n_blocks, PAIRS, 2]),
+                in1=table.rearrange("p w s (i two) -> p w s i two", two=2),
+                op=MULT,
+            )
 
-        def two_products(a_part, b_part, u, cd, dc):
-            shape = [P, u.shape[1], PAIRS, 2]
-            nc.vector.tensor_tensor(out=a_part, in0=u[:, :, :, 0:1].to_broadcast(shape), in1=cd, op=MULT)
-            nc.vector.tensor_tensor(out=b_part, in0=u[:, :, :, 1:2].to_broadcast(shape), in1=dc, op=MULT)
-
-        def add_up(a_part, b_part, engine):
-            flat_a = a_part[:].rearrange("p s t f -> p (s t f)")
-            engine.tensor_tensor(out=flat_a, in0=flat_a, in1=b_part[:].rearrange("p s t f -> p (s t f)"), op=ADD)
+        def add_up(parts, engine):
+            flat_a = parts[:, 0, :, :, :].rearrange("p s t f -> p (s t f)")
+            engine.tensor_tensor(
+                out=flat_a, in0=flat_a, in1=parts[:, 1, :, :, :].rearrange("p s t f -> p (s t f)"), op=ADD
+            )
 
         def queries(bank, pair, engine):
             blocks = slice(BLOCKS * bank, BLOCKS * (bank + 1))
-            a_part = results.tile([P, BLOCKS, PAIR, HD], F32, name="q_a")
-            b_part = products.tile([P, BLOCKS, PAIR, HD], F32, name="q_b")
+            parts = results.tile([P, 2, BLOCKS, PAIR, HD], F32, name="q_parts")
             for place in range(PAIR):
                 acc = project(PAIR * pair + place, bank)
-                two_products(
-                    by_pairs(a_part[:, :, place, :]),
-                    by_pairs(b_part[:, :, place, :]),
-                    by_pairs(acc[:].rearrange("p (s f) -> p s f", f=HD)),
-                    by_pairs(cd_q[:, blocks, :]),
-                    by_pairs(dc_q[:, blocks, :]),
-                )
-            add_up(a_part, b_part, engine)
-            nc.sync.dma_start(out=q_rows[:, blocks, PAIR * pair : PAIR * (pair + 1), :], in_=a_part[:])
+                both_products(parts[:, :, :, place, :], acc[:], table_q[:, :, blocks, :])
+            add_up(parts, engine)
+            nc.sync.dma_start(out=q_rows[:, blocks, PAIR * pair : PAIR * (pair + 1), :], in_=parts[:, 0, :, :, :])
 
         QUAD = 4
 
         def keys_and_values(quad):
-            a_part = results.tile([P, GROUPS, QUAD, HD], F32, name="k_a")
-            b_part = products.tile([P, GROUPS, QUAD, HD], F32, name="k_b")
+            parts = results.tile([P, 2, GROUPS, QUAD, HD], F32, name="k_parts")
             values = results.tile([P, GROUPS, QUAD, HD], F32, name="v")
             for place in range(QUAD):
                 r = QUAD * quad + place
                 acc = project(r, Q_BANKS)
-                kv = acc[:].rearrange("p (g two f) -> p g two f", two=2, f=HD)
-                two_products(
-                    by_pairs(a_part[:, :, place, :]),
-                    by_pairs(b_part[:, :, place, :]),
-                    by_pairs(kv[:, :, 0, :]),
-                    by_pairs(cd_k[:, :, r // 2, :]),
-                    by_pairs(dc_k[:, :, r // 2, :]),
+                both_products(parts[:, :, :, place, :], acc[:, 0 : GROUPS * HD], table_k[:, :, :, r // 2, :])
+                nc.scalar.copy(
+                    out=values[:, :, place, :], in_=acc[:, GROUPS * HD : BANK].rearrange("p (g f) -> p g f", f=HD)
                 )
-                nc.scalar.copy(out=values[:, :, place, :], in_=kv[:, :, 1, :])
             tiles = slice(QUAD * quad, QUAD * (quad + 1))
             nc.sync.dma_start(out=v_rows[:, :, tiles, :], in_=values[:])
-            add_up(a_part, b_part, nc.gpsimd)
-            nc.sync.dma_start(out=k_rows[:, :, tiles, :], in_=a_part[:])
+            add_up(parts, nc.gpsimd)
+            nc.sync.dma_start(out=k_rows[:, :, tiles, :], in_=parts[:, 0, :, :, :])
 
         pairs = TILES // PAIR
         quantise_tiles(0, 1)
@@ -233,7 +223,9 @@ def tile_causalselfattentiongqa_pa_kernel(
             queries(0, pair, nc.gpsimd)
             if pair + 2 < pairs:
                 quantise_tiles(PAIR * (pair + 2), PAIR)
-        turned_table_on_scalar(dc_k[:].rearrange("p g j f -> p (g j f)"), cd_k[:].rearrange("p g j f -> p (g j f)"))
+        turned_table_on_scalar(
+            table_k[:, 1, :, :, :].rearrange("p g j f -> p (g j f)"), table_k[:, 0, :, :, :].rearrange("p g j f -> p (g j f)")
+        )
         for quad in range(TILES // QUAD):
             keys_and_values(quad)
         for pair in range(pairs):

@@ -40,7 +40,7 @@ def tile_causalselfattentiongqa_pa_kernel(
     with ExitStack() as ctx:
         keep = ctx.enter_context(tc.tile_pool(name="keep", bufs=1))
         stage = ctx.enter_context(tc.tile_pool(name="stage", bufs=3))
-        results = ctx.enter_context(tc.tile_pool(name="results", bufs=4))
+        results = ctx.enter_context(tc.tile_pool(name="results", bufs=8))
         flipped = ctx.enter_context(tc.psum_pool(name="flipped", bufs=2))
         sums = ctx.enter_context(tc.psum_pool(name="sums", bufs=6))
 

@@ -195,6 +195,12 @@ def tile_causalselfattentiongqa_pa_kernel(
             for place in range(PAIR):
                 acc = project(PAIR * pair + place, bank)
                 both_products(parts[:, :, :, place, :], acc[:], table_q[:, :, blocks, :])
+            if engine is not None:
+                finish(parts, bank, pair, engine)
+            return parts
+
+        def finish(parts, bank, pair, engine):
+            blocks = slice(BLOCKS * bank, BLOCKS * (bank + 1))
             add_up(parts, engine)
             nc.sync.dma_start(out=q_rows[:, blocks, PAIR * pair : PAIR * (pair + 1), :], in_=parts[:, 0, :, :, :])
 
@@ -228,5 +234,8 @@ def tile_causalselfattentiongqa_pa_kernel(
         )
         for quad in range(TILES // QUAD):
             keys_and_values(quad)
+        late = []
         for pair in range(pairs):
-            queries(1, pair, nc.vector if pair == pairs - 1 else nc.gpsimd)
+            late.append(queries(1, pair, nc.gpsimd if pair < pairs - 2 else None))
+        for pair in range(pairs - 2, pairs):
+            finish(late[pair], 1, pair, nc.vector)

@@ -65,6 +65,7 @@ def tile_causalselfattentiongqa_pa_kernel(
         table_q = keep.tile([P, 2, GROUPS * Q_SLOTS, HD], BF16)
         table_k = keep.tile([P, 2, GROUPS, TILES // 2, HD], BF16)
         identity = keep.tile([P, P], F32)
+        seen = keep.tile([P, 1], U32)
 
         nc.vector.memset(w_scales[:].bitcast(I32), 0)
         make_identity(nc, identity[:])
@@ -99,15 +100,13 @@ def tile_causalselfattentiongqa_pa_kernel(
             in_=freqs_cis.rearrange("(g p j) i c -> p g (j i c)", g=GROUPS, p=P),
         )
 
-        def turned_table(dc, cd):
+        def turned_table_on_vector(dc, cd):
             cd_pairs = cd.rearrange("p (n two) -> p n two", two=2)
             dc_pairs = dc.rearrange("p (n two) -> p n two", two=2)
-            nc.gpsimd.tensor_scalar(
+            nc.vector.tensor_scalar(
                 out=dc_pairs[:, :, 0:1], in0=cd_pairs[:, :, 1:2], scalar1=-1.0, scalar2=0.0, op0=MULT, op1=ADD
             )
-            nc.gpsimd.tensor_scalar(
-                out=dc_pairs[:, :, 1:2], in0=cd_pairs[:, :, 0:1], scalar1=1.0, scalar2=0.0, op0=MULT, op1=ADD
-            )
+            nc.vector.tensor_copy(out=dc_pairs[:, :, 1:2], in_=cd_pairs[:, :, 0:1])
 
         def turned_table_on_scalar(dc, cd):
             cd_pairs = cd.rearrange("p (n two) -> p n two", two=2)
@@ -115,9 +114,9 @@ def tile_causalselfattentiongqa_pa_kernel(
             nc.scalar.mul(out=dc_pairs[:, :, 0:1], in_=cd_pairs[:, :, 1:2], mul=-1.0)
             nc.scalar.copy(out=dc_pairs[:, :, 1:2], in_=cd_pairs[:, :, 0:1])
 
-        for bank in range(Q_BANKS):
+        def turned_q(bank, how):
             blocks = slice(BLOCKS * bank, BLOCKS * (bank + 1))
-            turned_table(
+            how(
                 table_q[:, 1, blocks, :].rearrange("p s f -> p (s f)"),
                 table_q[:, 0, blocks, :].rearrange("p s f -> p (s f)"),
             )
@@ -223,12 +222,16 @@ def tile_causalselfattentiongqa_pa_kernel(
 
         pairs = TILES // PAIR
         quantise_tiles(0, 1)
+        turned_q(0, turned_table_on_vector)
         quantise_tiles(1, 1)
         quantise_tiles(2, 2)
         for pair in range(pairs):
-            queries(0, pair, nc.gpsimd)
+            parts = queries(0, pair, None)
             if pair + 2 < pairs:
                 quantise_tiles(PAIR * (pair + 2), PAIR)
+                nc.gpsimd.tensor_copy(out=seen[:], in_=x_codes[:, PAIR * (pair + 2), 0:1])
+            finish(parts, 0, pair, nc.gpsimd)
+        turned_q(1, turned_table_on_scalar)
         turned_table_on_scalar(
             table_k[:, 1, :, :, :].rearrange("p g j f -> p (g j f)"), table_k[:, 0, :, :, :].rearrange("p g j f -> p (g j f)")
         )

@@ -33,6 +33,20 @@ PAIR = 2
 FLOPS = 2 * TOKENS * K * COLS
 
 
+LOADS = [(1, 1), "W0", "SC", "tq0", "w", "tq1", (2, 2), "tk", (4, 2), (6, 2)]
+STEPS = [
+    ("S", 0, 1), ("Z", 0, 1), ("S", 1, 1), ("Z", 1, 1), ("N", 0), ("M", 0, 0), ("M", 1, 0), ("N", 1), ("M", 0, 1), ("M", 1, 1), ("S", 2, 2),
+    ("P", 0, 0), ("P", 1, 0), ("A", 0, 0, "g"), ("P", 0, 1), ("P", 1, 1), ("Z", 2, 2), ("H", 2), ("A", 0, 1, "g"), ("N", 2), ("M", 0, 2), ("M", 1, 2), ("S", 4, 2),
+    ("M", 2, 0), ("M", 3, 0), ("S", 6, 2), ("P", 0, 2), ("P", 1, 2),
+    ("M", 2, 1), ("M", 3, 1), ("P", 2, 0), ("P", 3, 0), ("Z", 4, 2), ("Z", 6, 2), ("H", 6), ("A", 1, 0, "g"),
+    ("M", 2, 2), ("M", 3, 2), ("P", 2, 1), ("P", 3, 1), ("A", 1, 1, "g"), ("M", 4, 0), ("M", 5, 0), ("P", 2, 2), ("P", 3, 2), ("A", 0, 2, "g"),
+    ("M", 4, 1), ("M", 5, 1), ("P", 4, 0), ("P", 5, 0), ("A", 2, 0, "g"),
+    ("M", 4, 2), ("M", 5, 2), ("P", 4, 1), ("P", 5, 1), ("A", 2, 1, "g"), ("M", 6, 2), ("M", 7, 2), ("P", 4, 2), ("P", 5, 2),
+    ("M", 6, 0), ("M", 7, 0), ("P", 6, 2), ("P", 7, 2), ("A", 1, 2, "g"), ("M", 6, 1), ("M", 7, 1), ("P", 6, 0), ("P", 7, 0),
+    ("P", 6, 1), ("P", 7, 1), ("A", 3, 0, "v"), ("A", 3, 1, "v"),
+]
+
+
 def tile_causalselfattentiongqa_pa_kernel(
     tc, x, freqs_cis, W_attn_words, W_attn_scales, out_0, out_1, out_2
 ):
@@ -41,19 +55,15 @@ def tile_causalselfattentiongqa_pa_kernel(
         keep = ctx.enter_context(tc.tile_pool(name="keep", bufs=1))
         stage = ctx.enter_context(tc.tile_pool(name="stage", bufs=3))
         results = ctx.enter_context(tc.tile_pool(name="results", bufs=8))
+        kv_results = ctx.enter_context(tc.tile_pool(name="kv_results", bufs=2))
         flipped = ctx.enter_context(tc.psum_pool(name="flipped", bufs=2))
         sums = ctx.enter_context(tc.psum_pool(name="sums", bufs=6))
+        ctx.enter_context(tc.manual_schedule())
 
         x_view = x.rearrange("o (p r) k -> (o p) r k", r=TILES)
-        q_rows = out_0.rearrange("o n h f -> (o n h) f").rearrange(
-            "(s p r) f -> p s r f", p=P, r=TILES
-        )
-        k_rows = out_1.rearrange("o n h f -> (o n h) f").rearrange(
-            "(g p r) f -> p g r f", p=P, r=TILES
-        )
-        v_rows = out_2.rearrange("o n h f -> (o n h) f").rearrange(
-            "(g p r) f -> p g r f", p=P, r=TILES
-        )
+        q_rows = out_0.rearrange("o n h f -> (o n h) f").rearrange("(s p r) f -> p s r f", p=P, r=TILES)
+        k_rows = out_1.rearrange("o n h f -> (o n h) f").rearrange("(g p r) f -> p g r f", p=P, r=TILES)
+        v_rows = out_2.rearrange("o n h f -> (o n h) f").rearrange("(g p r) f -> p g r f", p=P, r=TILES)
         words_i32 = W_attn_words.bitcast(I32).rearrange("c p n -> p c n")
         scales_i32 = W_attn_scales.bitcast(I32)
 
@@ -62,10 +72,13 @@ def tile_causalselfattentiongqa_pa_kernel(
         x_scales = keep.tile([P, TILES, PASSES * P], U8, align_bytes=64)
         w_words = keep.tile([P, PASSES, 2 * COLS], U8, align_bytes=64)
         w_scales = keep.tile([P, PASSES, COLS], U8, align_bytes=64)
-        table_q = keep.tile([P, 2, GROUPS * Q_SLOTS, HD], BF16)
-        table_k = keep.tile([P, 2, GROUPS, TILES // 2, HD], BF16)
-        identity = keep.tile([P, P], F32)
+        table_q0 = keep.tile([P, 2, BANK], BF16)
+        table_q1 = keep.tile([P, 2, BANK], BF16)
+        table_q = [table_q0, table_q1]
+        K_LEN = GROUPS * (TILES // 2) * HD
+        table_k = keep.tile([P, 2 * K_LEN + 4], BF16)
         seen = keep.tile([P, 1], U32)
+        identity = keep.tile([P, P], F32)
 
         nc.vector.memset(w_scales[:].bitcast(I32), 0)
         make_identity(nc, identity[:])
@@ -84,64 +97,85 @@ def tile_causalselfattentiongqa_pa_kernel(
         fc_q = freqs_cis.rearrange("(s p) i c -> p s (i c)", p=P)
 
         load_x(0, 1)
-        load_words(0, q_bytes)
-        for quadrant in range(4):
+
+        def load_scales():
+            for quadrant in range(4):
+                nc.sync.dma_start(
+                    out=w_scales[32 * quadrant : 32 * quadrant + 4, :, :].bitcast(I32),
+                    in_=scales_i32[:, 4 * quadrant : 4 * quadrant + 4, :].rearrange("g r n -> r g n"),
+                )
+
+        def load_tq(bank):
             nc.sync.dma_start(
-                out=w_scales[32 * quadrant : 32 * quadrant + 4, :, :].bitcast(I32),
-                in_=scales_i32[:, 4 * quadrant : 4 * quadrant + 4, :].rearrange("g r n -> r g n"),
+                out=table_q[bank][:, 1, :].rearrange("p (s f) -> p s f", f=HD),
+                in_=fc_q[:, BLOCKS * bank : BLOCKS * (bank + 1), :],
             )
-        nc.sync.dma_start(out=table_q[:, 0, :, :], in_=fc_q)
-        load_x(1, 1)
-        load_x(2, 2)
-        load_x(4, 4)
-        load_words(q_bytes, 2 * COLS - q_bytes)
-        nc.sync.dma_start(
-            out=table_k[:, 0, :, :, :].rearrange("p g j f -> p g (j f)"),
-            in_=freqs_cis.rearrange("(g p j) i c -> p g (j i c)", g=GROUPS, p=P),
+
+        def load_tk():
+            nc.sync.dma_start(
+                out=table_k[:, K_LEN + 2 : 2 * K_LEN + 2].rearrange("p (g n) -> p g n", g=GROUPS),
+                in_=freqs_cis.rearrange("(g p j) i c -> p g (j i c)", g=GROUPS, p=P),
+            )
+
+        for what in LOADS:
+            if what == "tq0":
+                load_tq(0)
+            elif what == "tq1":
+                load_tq(1)
+            elif what == "W0":
+                load_words(0, q_bytes)
+            elif what == "SC":
+                load_scales()
+            elif what == "tk":
+                load_tk()
+            elif what == "w":
+                load_words(q_bytes, 2 * COLS - q_bytes)
+            else:
+                load_x(what[0], what[1])
+
+        def negate(bank):
+            nc.scalar.mul(out=table_q[bank][:, 0, :], in_=table_q[bank][:, 1, :], mul=-1.0)
+
+        def turned_q(bank):
+            shifted = (
+                table_q[bank][:].rearrange("p w l -> p (w l)")[:, 1 : 2 * BANK - 1].rearrange("p (two j) -> p two j", two=2)
+            )
+            return shifted[:, :, 0 : BANK - 1 : 2].rearrange("p two (s i) -> p s i two", i=PAIRS)
+
+        def negate_k():
+            nc.scalar.mul(out=table_k[:, 0:K_LEN], in_=table_k[:, K_LEN + 2 : 2 * K_LEN + 2], mul=-1.0)
+
+        cd_k = table_k[:, K_LEN + 2 : 2 * K_LEN + 2].rearrange("p (g j i two) -> p j g i two", g=GROUPS, i=PAIRS, two=2)
+        dc_k = (
+            table_k[:, 1 : 2 * K_LEN + 3]
+            .rearrange("p (two n) -> p two n", two=2)[:, :, 0:K_LEN]
+            .rearrange("p two (g j i e) -> p e j g i two", g=GROUPS, i=PAIRS, e=2)[:, 0]
         )
 
-        def turned_table_on_vector(dc, cd):
-            cd_pairs = cd.rearrange("p (n two) -> p n two", two=2)
-            dc_pairs = dc.rearrange("p (n two) -> p n two", two=2)
-            nc.vector.tensor_scalar(
-                out=dc_pairs[:, :, 0:1], in0=cd_pairs[:, :, 1:2], scalar1=-1.0, scalar2=0.0, op0=MULT, op1=ADD
-            )
-            nc.vector.tensor_copy(out=dc_pairs[:, :, 1:2], in_=cd_pairs[:, :, 0:1])
+        staged = {}
 
-        def turned_table_on_scalar(dc, cd):
-            cd_pairs = cd.rearrange("p (n two) -> p n two", two=2)
-            dc_pairs = dc.rearrange("p (n two) -> p n two", two=2)
-            nc.scalar.mul(out=dc_pairs[:, :, 0:1], in_=cd_pairs[:, :, 1:2], mul=-1.0)
-            nc.scalar.copy(out=dc_pairs[:, :, 1:2], in_=cd_pairs[:, :, 0:1])
-
-        def turned_q(bank, how):
-            blocks = slice(BLOCKS * bank, BLOCKS * (bank + 1))
-            how(
-                table_q[:, 1, blocks, :].rearrange("p s f -> p (s f)"),
-                table_q[:, 0, blocks, :].rearrange("p s f -> p (s f)"),
-            )
-
-        def quantise_tiles(first_tile, count):
+        def stage_tiles(first_tile, count):
             grouped = stage.tile([P, count, PASSES * P * 4], BF16, align_bytes=64, name="grouped")
+            staged[first_tile] = grouped
             for n in range(count):
                 x_words = x_sb[:, first_tile + n, :].bitcast(F32)
                 turned = flipped.tile([P, PASSES, 2, P], F32, name="turned")
                 for c in range(PASSES):
                     for u in range(2):
                         nc.tensor.transpose(
-                            turned[:, c, u, :],
-                            x_words[:, K_PASS // 2 * c + u : K_PASS // 2 * (c + 1) : 2],
-                            identity[:],
+                            turned[:, c, u, :], x_words[:, K_PASS // 2 * c + u : K_PASS // 2 * (c + 1) : 2], identity[:]
                         )
                 nc.scalar.copy(
                     out=grouped[:, n, :].bitcast(F32).rearrange("p (c t u) -> p c t u", c=PASSES, u=2),
                     in_=turned[:].rearrange("p c u t -> p c t u"),
                 )
+
+        def quantise(first_tile, count):
             tiles = slice(first_tile, first_tile + count)
             nc.vector.quantize_mx(
                 out=x_codes[:, tiles, :].rearrange("p r w -> p (r w)").bitcast(FP8X4),
                 scales=x_scales[:, tiles, :].rearrange("p r w -> p (r w)"),
-                in_=grouped[:].rearrange("p r w -> p (r w)"),
+                in_=staged[first_tile][:].rearrange("p r w -> p (r w)"),
             )
 
         def multiply(acc, r, first_col, n_cols):
@@ -156,8 +190,11 @@ def tile_causalselfattentiongqa_pa_kernel(
                     stop=(c == PASSES - 1),
                 )
 
+        accs = {}
+
         def project(r, bank):
             acc = sums.tile([P, BANK], F32, name="acc")
+            accs[(r, bank)] = acc
             if bank < Q_BANKS:
                 multiply(acc[:], r, GROUP_COLS * bank, BANK)
             else:
@@ -169,18 +206,30 @@ def tile_causalselfattentiongqa_pa_kernel(
                             GROUP_COLS * g + HD * (Q_SLOTS + slot),
                             HD,
                         )
-            return acc
 
-        def both_products(parts, u, table):
-            n_blocks = parts.shape[2]
+        q_parts = {}
+
+        def product(r, bank, which):
+            pair, place = r // PAIR, r % PAIR
+            if (pair, bank) not in q_parts:
+                new_parts = results.tile([P, 2, BLOCKS, PAIR, HD], F32, name="q_parts")
+                q_parts[(pair, bank)] = new_parts
+            parts = q_parts[(pair, bank)]
+            u = accs[(r, bank)][:].rearrange("p (s i w) -> p w s i", i=PAIRS, w=2)
+            if which == 0:
+                table = table_q[bank][:, 1, :].rearrange("p (s i two) -> p s i two", i=PAIRS, two=2)
+            else:
+                table = turned_q(bank)
             nc.vector.tensor_tensor(
-                out=parts.rearrange("p w s (i two) -> p w s i two", two=2),
-                in0=u.rearrange("p (s i w) -> p w s i", i=PAIRS, w=2)
-                .unsqueeze(4)
-                .to_broadcast([P, 2, n_blocks, PAIRS, 2]),
-                in1=table.rearrange("p w s (i two) -> p w s i two", two=2),
+                out=parts[:, which, :, place, :].rearrange("p s (i two) -> p s i two", two=2),
+                in0=u[:, which, :, :].unsqueeze(3).to_broadcast([P, BLOCKS, PAIRS, 2]),
+                in1=table,
                 op=MULT,
             )
+
+        def both(r, bank):
+            product(r, bank, 0)
+            product(r, bank, 1)
 
         def add_up(parts, engine):
             flat_a = parts[:, 0, :, :, :].rearrange("p s t f -> p (s t f)")
@@ -188,57 +237,76 @@ def tile_causalselfattentiongqa_pa_kernel(
                 out=flat_a, in0=flat_a, in1=parts[:, 1, :, :, :].rearrange("p s t f -> p (s t f)"), op=ADD
             )
 
-        def queries(bank, pair, engine):
-            blocks = slice(BLOCKS * bank, BLOCKS * (bank + 1))
-            parts = results.tile([P, 2, BLOCKS, PAIR, HD], F32, name="q_parts")
-            for place in range(PAIR):
-                acc = project(PAIR * pair + place, bank)
-                both_products(parts[:, :, :, place, :], acc[:], table_q[:, :, blocks, :])
-            if engine is not None:
-                finish(parts, bank, pair, engine)
-            return parts
-
-        def finish(parts, bank, pair, engine):
+        def finish(pair, bank, engine):
+            parts = q_parts[(pair, bank)]
             blocks = slice(BLOCKS * bank, BLOCKS * (bank + 1))
             add_up(parts, engine)
             nc.sync.dma_start(out=q_rows[:, blocks, PAIR * pair : PAIR * (pair + 1), :], in_=parts[:, 0, :, :, :])
 
         QUAD = 4
 
-        def keys_and_values(quad):
-            parts = results.tile([P, 2, GROUPS, QUAD, HD], F32, name="k_parts")
-            values = results.tile([P, GROUPS, QUAD, HD], F32, name="v")
-            for place in range(QUAD):
-                r = QUAD * quad + place
-                acc = project(r, Q_BANKS)
-                both_products(parts[:, :, :, place, :], acc[:, 0 : GROUPS * HD], table_k[:, :, :, r // 2, :])
-                nc.scalar.copy(
-                    out=values[:, :, place, :], in_=acc[:, GROUPS * HD : BANK].rearrange("p (g f) -> p g f", f=HD)
-                )
-            tiles = slice(QUAD * quad, QUAD * (quad + 1))
-            nc.sync.dma_start(out=v_rows[:, :, tiles, :], in_=values[:])
-            add_up(parts, nc.gpsimd)
-            nc.sync.dma_start(out=k_rows[:, :, tiles, :], in_=parts[:, 0, :, :, :])
+        k_parts = {}
+        v_parts = {}
 
-        pairs = TILES // PAIR
-        quantise_tiles(0, 1)
-        turned_q(0, turned_table_on_vector)
-        quantise_tiles(1, 1)
-        quantise_tiles(2, 2)
-        for pair in range(pairs):
-            parts = queries(0, pair, None)
-            if pair + 2 < pairs:
-                quantise_tiles(PAIR * (pair + 2), PAIR)
-                nc.gpsimd.tensor_copy(out=seen[:], in_=x_codes[:, PAIR * (pair + 2), 0:1])
-            finish(parts, 0, pair, nc.gpsimd)
-        turned_q(1, turned_table_on_scalar)
-        turned_table_on_scalar(
-            table_k[:, 1, :, :, :].rearrange("p g j f -> p (g j f)"), table_k[:, 0, :, :, :].rearrange("p g j f -> p (g j f)")
-        )
-        for quad in range(TILES // QUAD):
-            keys_and_values(quad)
-        late = []
-        for pair in range(pairs):
-            late.append(queries(1, pair, nc.gpsimd if pair < pairs - 2 else None))
-        for pair in range(pairs - 2, pairs):
-            finish(late[pair], 1, pair, nc.vector)
+        def keys(r):
+            quad, place = r // QUAD, r % QUAD
+            if quad not in k_parts:
+                new_k = kv_results.tile([P, 2, GROUPS, QUAD, HD], F32, name="k_parts")
+                new_v = kv_results.tile([P, GROUPS, QUAD, HD], F32, name="v")
+                k_parts[quad] = new_k
+                v_parts[quad] = new_v
+            acc = accs[(r, Q_BANKS)]
+            u = acc[:, 0 : GROUPS * HD].rearrange("p (s i w) -> p w s i", i=PAIRS, w=2)
+            for which in range(2):
+                nc.vector.tensor_tensor(
+                    out=k_parts[quad][:, which, :, place, :].rearrange("p s (i two) -> p s i two", two=2),
+                    in0=u[:, which, :, :].unsqueeze(3).to_broadcast([P, GROUPS, PAIRS, 2]),
+                    in1=(cd_k if which == 0 else dc_k)[:, r // 2],
+                    op=MULT,
+                )
+            nc.scalar.copy(
+                out=v_parts[quad][:, :, place, :], in_=acc[:, GROUPS * HD : BANK].rearrange("p (g f) -> p g f", f=HD)
+            )
+            if place == QUAD - 1:
+                nc.sync.dma_start(out=v_rows[:, :, QUAD * quad : QUAD * (quad + 1), :], in_=v_parts[quad][:])
+
+        def finish_k(quad, engine):
+            add_up(k_parts[quad], engine)
+            nc.sync.dma_start(out=k_rows[:, :, QUAD * quad : QUAD * (quad + 1), :], in_=k_parts[quad][:, 0, :, :, :])
+
+        engines = {"g": nc.gpsimd, "v": nc.vector}
+        for step in STEPS:
+            op = step[0]
+            if op == "S":
+                stage_tiles(step[1], step[2])
+            elif op == "Z":
+                quantise(step[1], step[2])
+            elif op == "N":
+                if step[1] == 2:
+                    negate_k()
+                else:
+                    negate(step[1])
+            elif op == "M":
+                project(step[1], step[2])
+            elif op == "P":
+                if step[2] == 2:
+                    keys(step[1])
+                else:
+                    both(step[1], step[2])
+            elif op == "A":
+                if step[2] == 2:
+                    finish_k(step[1], engines[step[3]])
+                else:
+                    finish(step[1], step[2], engines[step[3]])
+            elif op == "a":
+                r, bank = step[1], step[2]
+                parts = q_parts[(r // PAIR, bank)]
+                nc.vector.tensor_tensor(
+                    out=parts[:, 0, :, r % PAIR, :], in0=parts[:, 0, :, r % PAIR, :], in1=parts[:, 1, :, r % PAIR, :], op=ADD
+                )
+                if r % PAIR == PAIR - 1:
+                    nc.sync.dma_start(
+                        out=q_rows[:, BLOCKS * bank : BLOCKS * (bank + 1), r - 1 : r + 1, :], in_=parts[:, 0, :, :, :]
+                    )
+            elif op == "H":
+                nc.gpsimd.tensor_copy(out=seen[:], in_=x_codes[:, step[1], 0:1])

@@ -35,7 +35,7 @@ FLOPS = 2 * TOKENS * K * COLS
 
 LOADS = [(1, 1), "W0", "SC", "tq0", "w", "tq1", (2, 2), "tk", (4, 2), (6, 2)]
 STEPS = [
-    ("S", 0, 1), ("Z", 0, 1), ("S", 1, 1), ("Z", 1, 1), ("N", 0), ("M", 0, 0), ("M", 1, 0), ("N", 1), ("M", 0, 1), ("M", 1, 1), ("S", 2, 2),
+    ("D", 3), ("Sp", 0, 0), ("Zp", 0, 0), ("Sp", 0, 1), ("Zp", 0, 1), ("S", 1, 1), ("N", 0), ("M", 0, 0), ("Z", 1, 1), ("M", 1, 0), ("N", 1), ("M", 0, 1), ("M", 1, 1), ("S", 2, 2),
     ("P", 0, 0), ("P", 1, 0), ("A", 0, 0, "g"), ("P", 0, 1), ("P", 1, 1), ("Z", 2, 2), ("H", 2), ("A", 0, 1, "g"), ("N", 2), ("M", 0, 2), ("M", 1, 2), ("S", 4, 2),
     ("M", 2, 0), ("M", 3, 0), ("S", 6, 2), ("P", 0, 2), ("P", 1, 2),
     ("M", 2, 1), ("M", 3, 1), ("P", 2, 0), ("P", 3, 0), ("Z", 4, 2), ("Z", 6, 2), ("H", 6), ("A", 1, 0, "g"),
@@ -70,7 +70,8 @@ def tile_causalselfattentiongqa_pa_kernel(
         x_sb = keep.tile([P, TILES, K], BF16)
         x_codes = keep.tile([P, TILES, PASSES * P], U32, align_bytes=64)
         x_scales = keep.tile([P, TILES, PASSES * P], U8, align_bytes=64)
-        w_words = keep.tile([P, PASSES, 2 * COLS], U8, align_bytes=64)
+        w_first = keep.tile([P, PASSES, 2 * BANK], U8, align_bytes=64)
+        w_rest = keep.tile([P, PASSES, 2 * (COLS - BANK)], U8, align_bytes=64)
         w_scales = keep.tile([P, PASSES, COLS], U8, align_bytes=64)
         table_q0 = keep.tile([P, 2, BANK], BF16)
         table_q1 = keep.tile([P, 2, BANK], BF16)
@@ -81,16 +82,17 @@ def tile_causalselfattentiongqa_pa_kernel(
         identity = keep.tile([P, P], F32)
 
         nc.vector.memset(w_scales[:].bitcast(I32), 0)
+        zeros = keep.tile([P, BANK], BF16)
+        nc.vector.memset(zeros[:], 0.0)
         make_identity(nc, identity[:])
 
         def load_x(first_tile, count):
             tiles = slice(first_tile, first_tile + count)
             nc.sync.dma_start(out=x_sb[:, tiles, :], in_=x_view[:, tiles, :])
 
-        def load_words(first_byte, n_bytes):
+        def load_words(tile, first_byte, n_bytes):
             nc.sync.dma_start(
-                out=w_words[:, :, first_byte : first_byte + n_bytes].bitcast(I32),
-                in_=words_i32[:, :, first_byte // 4 : (first_byte + n_bytes) // 4],
+                out=tile[:].bitcast(I32), in_=words_i32[:, :, first_byte // 4 : (first_byte + n_bytes) // 4]
             )
 
         q_bytes = 2 * Q_SLOTS * HD
@@ -123,13 +125,13 @@ def tile_causalselfattentiongqa_pa_kernel(
             elif what == "tq1":
                 load_tq(1)
             elif what == "W0":
-                load_words(0, q_bytes)
+                load_words(w_first, 0, q_bytes)
             elif what == "SC":
                 load_scales()
             elif what == "tk":
                 load_tk()
             elif what == "w":
-                load_words(q_bytes, 2 * COLS - q_bytes)
+                load_words(w_rest, q_bytes, 2 * COLS - q_bytes)
             else:
                 load_x(what[0], what[1])
 
@@ -170,6 +172,32 @@ def tile_causalselfattentiongqa_pa_kernel(
                     in_=turned[:].rearrange("p c u t -> p c t u"),
                 )
 
+        whole = {}
+
+        def stage_pass(r, c):
+            if r not in staged:
+                first = stage.tile([P, 1, PASSES * P * 4], BF16, align_bytes=64, name="grouped")
+                staged[r] = first
+                x_words = x_sb[:, r, :].bitcast(F32)
+                turned = flipped.tile([P, PASSES, 2, P], F32, name="turned")
+                whole[r] = turned
+                for cc in range(PASSES):
+                    for u in range(2):
+                        nc.tensor.transpose(
+                            turned[:, cc, u, :], x_words[:, K_PASS // 2 * cc + u : K_PASS // 2 * (cc + 1) : 2], identity[:]
+                        )
+            nc.scalar.copy(
+                out=staged[r][:, 0, K_PASS * c : K_PASS * (c + 1)].bitcast(F32).rearrange("p (t u) -> p t u", u=2),
+                in_=whole[r][:, c, :, :].rearrange("p u t -> p t u"),
+            )
+
+        def quantise_pass(r, c):
+            nc.vector.quantize_mx(
+                out=x_codes[:, r, P * c : P * (c + 1)].bitcast(FP8X4),
+                scales=x_scales[:, r, P * c : P * (c + 1)],
+                in_=staged[r][:, 0, K_PASS * c : K_PASS * (c + 1)],
+            )
+
         def quantise(first_tile, count):
             tiles = slice(first_tile, first_tile + count)
             nc.vector.quantize_mx(
@@ -179,12 +207,13 @@ def tile_causalselfattentiongqa_pa_kernel(
             )
 
         def multiply(acc, r, first_col, n_cols):
+            words, shift = (w_first, 0) if first_col < BANK else (w_rest, BANK)
             for c in range(PASSES):
                 nc.tensor.matmul_mx(
                     out=acc,
                     lhsT=x_codes[:, r, P * c : P * (c + 1)].bitcast(FP8X4),
                     lhsT_scale=x_scales[:, r, P * c : P * (c + 1)],
-                    rhs=w_words[:, c, 2 * first_col : 2 * (first_col + n_cols)].bitcast(FP4X4),
+                    rhs=words[:, c, 2 * (first_col - shift) : 2 * (first_col - shift + n_cols)].bitcast(FP4X4),
                     rhs_scale=w_scales[:, c, first_col : first_col + n_cols],
                     start=(c == 0),
                     stop=(c == PASSES - 1),
@@ -274,6 +303,34 @@ def tile_causalselfattentiongqa_pa_kernel(
             add_up(k_parts[quad], engine)
             nc.sync.dma_start(out=k_rows[:, :, QUAD * quad : QUAD * (quad + 1), :], in_=k_parts[quad][:, 0, :, :, :])
 
+        def add_k_pair(pair, engine):
+            parts = k_parts[pair // 2]
+            places = slice(PAIR * (pair % 2), PAIR * (pair % 2) + PAIR)
+            engine.tensor_tensor(
+                out=parts[:, 0, :, places, :].rearrange("p g t f -> p g (t f)"),
+                in0=parts[:, 0, :, places, :].rearrange("p g t f -> p g (t f)"),
+                in1=parts[:, 1, :, places, :].rearrange("p g t f -> p g (t f)"),
+                op=ADD,
+            )
+            if pair % 2 == 1:
+                quad = pair // 2
+                nc.sync.dma_start(out=k_rows[:, :, QUAD * quad : QUAD * (quad + 1), :], in_=parts[:, 0, :, :, :])
+
+        def finish_half(pair, bank, half, engine):
+            parts = q_parts[(pair, bank)]
+            some = slice(BLOCKS // 2 * half, BLOCKS // 2 * (half + 1))
+            engine.tensor_tensor(
+                out=parts[:, 0, some, :, :].rearrange("p s t f -> p (s t f)"),
+                in0=parts[:, 0, some, :, :].rearrange("p s t f -> p (s t f)"),
+                in1=parts[:, 1, some, :, :].rearrange("p s t f -> p (s t f)"),
+                op=ADD,
+            )
+            first_block = BLOCKS * bank + BLOCKS // 2 * half
+            nc.sync.dma_start(
+                out=q_rows[:, first_block : first_block + BLOCKS // 2, PAIR * pair : PAIR * (pair + 1), :],
+                in_=parts[:, 0, some, :, :],
+            )
+
         engines = {"g": nc.gpsimd, "v": nc.vector}
         for step in STEPS:
             op = step[0]
@@ -308,5 +365,17 @@ def tile_causalselfattentiongqa_pa_kernel(
                     nc.sync.dma_start(
                         out=q_rows[:, BLOCKS * bank : BLOCKS * (bank + 1), r - 1 : r + 1, :], in_=parts[:, 0, :, :, :]
                     )
+            elif op == "Sp":
+                stage_pass(step[1], step[2])
+            elif op == "Zp":
+                quantise_pass(step[1], step[2])
+            elif op == "Ak":
+                add_k_pair(step[1], engines[step[2]])
+            elif op == "Ah":
+                finish_half(step[1], step[2], step[3], engines[step[4]])
+            elif op == "D":
+                waste = sums.tile([P, BANK], F32, name="acc")
+                for n in range(step[1]):
+                    nc.tensor.matmul(out=waste[:], lhsT=zeros[:, 0:P], rhs=zeros[:], start=True, stop=True)
             elif op == "H":
                 nc.gpsimd.tensor_copy(out=seen[:], in_=x_codes[:, step[1], 0:1])

@@ -37,9 +37,9 @@ LOADS = [(1, 1), "W0", "SC", "tq0", "w", "tq1", (2, 2), "tk", (4, 2), (6, 2)]
 STEPS = [
     ("D", 3), ("Sp", 0, 0), ("Zp", 0, 0), ("Sp", 0, 1), ("Zp", 0, 1), ("S", 1, 1), ("N", 0), ("M", 0, 0), ("Z", 1, 1), ("M", 1, 0), ("N", 1), ("M", 0, 1), ("M", 1, 1), ("S", 2, 2),
     ("P", 0, 0), ("P", 1, 0), ("A", 0, 0, "g"), ("P", 0, 1), ("P", 1, 1), ("Z", 2, 2), ("H", 2), ("A", 0, 1, "g"), ("N", 2), ("M", 0, 2), ("M", 1, 2), ("S", 4, 2),
-    ("M", 2, 0), ("M", 3, 0), ("S", 6, 2), ("P", 0, 2), ("P", 1, 2),
+    ("M", 2, 0), ("M", 3, 0), ("S", 6, 2), ("P", 0, 2), ("P", 1, 2), ("Ak", 0, "g"),
     ("M", 2, 1), ("M", 3, 1), ("P", 2, 0), ("P", 3, 0), ("Z", 4, 2), ("Z", 6, 2), ("H", 6), ("A", 1, 0, "g"),
-    ("M", 2, 2), ("M", 3, 2), ("P", 2, 1), ("P", 3, 1), ("A", 1, 1, "g"), ("M", 4, 0), ("M", 5, 0), ("P", 2, 2), ("P", 3, 2), ("A", 0, 2, "g"),
+    ("M", 2, 2), ("M", 3, 2), ("P", 2, 1), ("P", 3, 1), ("A", 1, 1, "g"), ("M", 4, 0), ("M", 5, 0), ("P", 2, 2), ("P", 3, 2), ("Ak", 1, "g"),
     ("M", 4, 1), ("M", 5, 1), ("P", 4, 0), ("P", 5, 0), ("A", 2, 0, "g"),
     ("M", 4, 2), ("M", 5, 2), ("P", 4, 1), ("P", 5, 1), ("A", 2, 1, "g"), ("M", 6, 2), ("M", 7, 2), ("P", 4, 2), ("P", 5, 2),
     ("M", 6, 0), ("M", 7, 0), ("P", 6, 2), ("P", 7, 2), ("A", 1, 2, "g"), ("M", 6, 1), ("M", 7, 1), ("P", 6, 0), ("P", 7, 0),

@@ -33,7 +33,7 @@ PAIR = 2
 FLOPS = 2 * TOKENS * K * COLS
 
 
-LOADS = [(1, 1), "W0", "SC", "tq0", "w", "tq1", (2, 2), "tk", (4, 2), (6, 2)]
+LOADS = [(1, 1), "W0", "SC0", "tq0", "w", "SC1", "tq1", (2, 2), "tk", (4, 2), (6, 2)]
 STEPS = [
     ("D", 3), ("Sp", 0, 0), ("Zp", 0, 0), ("Sp", 0, 1), ("Zp", 0, 1), ("S", 1, 1), ("N", 0), ("M", 0, 0), ("Z", 1, 1), ("M", 1, 0), ("N", 1), ("M", 0, 1), ("M", 1, 1), ("S", 2, 2),
     ("P", 0, 0), ("P", 1, 0), ("A", 0, 0, "g"), ("P", 0, 1), ("P", 1, 1), ("Z", 2, 2), ("H", 2), ("A", 0, 1, "g"), ("N", 2), ("M", 0, 2), ("M", 1, 2), ("S", 4, 2),
@@ -72,7 +72,8 @@ def tile_causalselfattentiongqa_pa_kernel(
         x_scales = keep.tile([P, TILES, PASSES * P], U8, align_bytes=64)
         w_first = keep.tile([P, PASSES, 2 * BANK], U8, align_bytes=64)
         w_rest = keep.tile([P, PASSES, 2 * (COLS - BANK)], U8, align_bytes=64)
-        w_scales = keep.tile([P, PASSES, COLS], U8, align_bytes=64)
+        s_first = keep.tile([P, PASSES, BANK], U8, align_bytes=64)
+        s_rest = keep.tile([P, PASSES, COLS - BANK], U8, align_bytes=64)
         table_q0 = keep.tile([P, 2, BANK], BF16)
         table_q1 = keep.tile([P, 2, BANK], BF16)
         table_q = [table_q0, table_q1]
@@ -81,7 +82,8 @@ def tile_causalselfattentiongqa_pa_kernel(
         seen = keep.tile([P, 1], U32)
         identity = keep.tile([P, P], F32)
 
-        nc.vector.memset(w_scales[:].bitcast(I32), 0)
+        nc.vector.memset(s_first[:].bitcast(I32), 0)
+        nc.vector.memset(s_rest[:].bitcast(I32), 0)
         zeros = keep.tile([P, BANK], BF16)
         nc.vector.memset(zeros[:], 0.0)
         make_identity(nc, identity[:])
@@ -100,11 +102,13 @@ def tile_causalselfattentiongqa_pa_kernel(
 
         load_x(0, 1)
 
-        def load_scales():
+        def load_scales(tile, first_col, n_cols):
             for quadrant in range(4):
                 nc.sync.dma_start(
-                    out=w_scales[32 * quadrant : 32 * quadrant + 4, :, :].bitcast(I32),
-                    in_=scales_i32[:, 4 * quadrant : 4 * quadrant + 4, :].rearrange("g r n -> r g n"),
+                    out=tile[32 * quadrant : 32 * quadrant + 4, :, :].bitcast(I32),
+                    in_=scales_i32[:, 4 * quadrant : 4 * quadrant + 4, first_col // 4 : (first_col + n_cols) // 4].rearrange(
+                        "g r n -> r g n"
+                    ),
                 )
 
         def load_tq(bank):
@@ -126,8 +130,10 @@ def tile_causalselfattentiongqa_pa_kernel(
                 load_tq(1)
             elif what == "W0":
                 load_words(w_first, 0, q_bytes)
-            elif what == "SC":
-                load_scales()
+            elif what == "SC0":
+                load_scales(s_first, 0, BANK)
+            elif what == "SC1":
+                load_scales(s_rest, BANK, COLS - BANK)
             elif what == "tk":
                 load_tk()
             elif what == "w":
@@ -207,14 +213,14 @@ def tile_causalselfattentiongqa_pa_kernel(
             )
 
         def multiply(acc, r, first_col, n_cols):
-            words, shift = (w_first, 0) if first_col < BANK else (w_rest, BANK)
+            words, scale_bytes, shift = (w_first, s_first, 0) if first_col < BANK else (w_rest, s_rest, BANK)
             for c in range(PASSES):
                 nc.tensor.matmul_mx(
                     out=acc,
                     lhsT=x_codes[:, r, P * c : P * (c + 1)].bitcast(FP8X4),
                     lhsT_scale=x_scales[:, r, P * c : P * (c + 1)],
                     rhs=words[:, c, 2 * (first_col - shift) : 2 * (first_col - shift + n_cols)].bitcast(FP4X4),
-                    rhs_scale=w_scales[:, c, first_col : first_col + n_cols],
+                    rhs_scale=scale_bytes[:, c, first_col - shift : first_col - shift + n_cols],
                     start=(c == 0),
                     stop=(c == PASSES - 1),
                 )

@@ -33,7 +33,7 @@ PAIR = 2
 FLOPS = 2 * TOKENS * K * COLS
 
 
-LOADS = [(1, 1), "W0", "SC0", "tq0", "w", "SC1", "tq1", (2, 2), "tk", (4, 2), (6, 2)]
+LOADS = [(1, 1), "SC0", "W0", "tq0", "w", "SC1", "tq1", (2, 2), "tk", (4, 2), (6, 2)]
 STEPS = [
     ("D", 3), ("Sp", 0, 0), ("Zp", 0, 0), ("Sp", 0, 1), ("Zp", 0, 1), ("S", 1, 1), ("N", 0), ("M", 0, 0), ("Z", 1, 1), ("M", 1, 0), ("N", 1), ("M", 0, 1), ("M", 1, 1), ("S", 2, 2),
     ("P", 0, 0), ("P", 1, 0), ("A", 0, 0, "g"), ("P", 0, 1), ("P", 1, 1), ("Z", 2, 2), ("H", 2), ("A", 0, 1, "g"), ("N", 2), ("M", 0, 2), ("M", 1, 2), ("S", 4, 2),
@@ -43,7 +43,7 @@ STEPS = [
     ("M", 4, 1), ("M", 5, 1), ("P", 4, 0), ("P", 5, 0), ("A", 2, 0, "g"),
     ("M", 4, 2), ("M", 5, 2), ("P", 4, 1), ("P", 5, 1), ("A", 2, 1, "g"), ("M", 6, 2), ("M", 7, 2), ("P", 4, 2), ("P", 5, 2),
     ("M", 6, 0), ("M", 7, 0), ("P", 6, 2), ("P", 7, 2), ("A", 1, 2, "g"), ("M", 6, 1), ("M", 7, 1), ("P", 6, 0), ("P", 7, 0),
-    ("P", 6, 1), ("P", 7, 1), ("A", 3, 0, "v"), ("A", 3, 1, "v"),
+    ("P", 6, 1), ("P", 7, 1), ("Ah", 3, 0, 0, "v"), ("Ah", 3, 0, 1, "v"), ("Ah", 3, 1, 0, "v"), ("Ah", 3, 1, 1, "v"),
 ]
 
 

@@ -35,15 +35,18 @@ FLOPS = 2 * TOKENS * K * COLS
 
 LOADS = [(1, 1), "SC0", "W0", "tq0", "w", "SC1", "tq1", (2, 2), "tk", (4, 2), (6, 2)]
 STEPS = [
-    ("D", 3), ("Sp", 0, 0), ("Zp", 0, 0), ("Sp", 0, 1), ("Zp", 0, 1), ("S", 1, 1), ("N", 0), ("M", 0, 0), ("Z", 1, 1), ("M", 1, 0), ("N", 1), ("M", 0, 1), ("M", 1, 1), ("S", 2, 2),
+    ("D", 3), ("Sp", 0, 0), ("Zp", 0, 0), ("Sp", 0, 1), ("Zp", 0, 1), ("S", 1, 1), ("N", 0), ("M", 0, 0), ("Z", 1, 1), ("M", 1, 0), ("N", 1), ("FD",), ("M", 0, 1), ("M", 1, 1), ("S", 2, 2),
     ("P", 0, 0), ("P", 1, 0), ("A", 0, 0, "g"), ("P", 0, 1), ("P", 1, 1), ("Z", 2, 2), ("H", 2), ("A", 0, 1, "g"), ("N", 2), ("M", 0, 2), ("M", 1, 2), ("S", 4, 2),
-    ("M", 2, 0), ("M", 3, 0), ("S", 6, 2), ("P", 0, 2), ("P", 1, 2), ("Ak", 0, "g"),
-    ("M", 2, 1), ("M", 3, 1), ("P", 2, 0), ("P", 3, 0), ("Z", 4, 2), ("Z", 6, 2), ("H", 6), ("A", 1, 0, "g"),
-    ("M", 2, 2), ("M", 3, 2), ("P", 2, 1), ("P", 3, 1), ("A", 1, 1, "g"), ("M", 4, 0), ("M", 5, 0), ("P", 2, 2), ("P", 3, 2), ("Ak", 1, "g"),
-    ("M", 4, 1), ("M", 5, 1), ("P", 4, 0), ("P", 5, 0), ("A", 2, 0, "g"),
-    ("M", 4, 2), ("M", 5, 2), ("P", 4, 1), ("P", 5, 1), ("A", 2, 1, "g"), ("M", 6, 2), ("M", 7, 2), ("P", 4, 2), ("P", 5, 2),
-    ("M", 6, 0), ("M", 7, 0), ("P", 6, 2), ("P", 7, 2), ("A", 1, 2, "g"), ("M", 6, 1), ("M", 7, 1), ("P", 6, 0), ("P", 7, 0),
-    ("P", 6, 1), ("P", 7, 1), ("Ah", 3, 0, 0, "v"), ("Ah", 3, 0, 1, "v"), ("Ah", 3, 1, 0, "v"), ("Ah", 3, 1, 1, "v"),
+    ("M", 2, 0), ("M", 3, 0), ("S", 6, 2), ("P", 0, 2), ("P", 1, 2),
+    ("M", 2, 2), ("M", 3, 2), ("P", 2, 0), ("P", 3, 0), ("Z", 4, 2), ("Z", 6, 2), ("H", 6), ("A", 1, 0, "g"),
+    ("M", 4, 0), ("M", 5, 0), ("FT",), ("P", 2, 2), ("P", 3, 2), ("A", 0, 2, "g"),
+    ("M", 4, 2), ("M", 5, 2), ("P", 4, 0), ("P", 5, 0), ("A", 2, 0, "g"),
+    ("FM", 0, 2), ("FM", 1, 2), ("P", 4, 2), ("P", 5, 2),
+    ("M", 6, 2), ("M", 7, 2), ("FP", 0), ("FP", 1),
+    ("FM", 2, 2), ("FM", 3, 2), ("FA", 0, 2), ("FA", 1, 2), ("P", 6, 2), ("P", 7, 2), ("A", 1, 2, "g"),
+    ("M", 6, 0), ("M", 7, 0), ("FP", 2), ("FP", 3),
+    ("M", 6, 1), ("M", 7, 1), ("FA", 2, 2), ("FA", 3, 2), ("P", 6, 0), ("P", 7, 0), ("Ah", 3, 0, 0, "g"),
+    ("P", 6, 1), ("P", 7, 1), ("Ah", 3, 0, 1, "v"), ("Ah", 3, 1, 0, "v"), ("Ah", 3, 1, 1, "v"),
 ]
 
 
@@ -56,6 +59,7 @@ def tile_causalselfattentiongqa_pa_kernel(
         stage = ctx.enter_context(tc.tile_pool(name="stage", bufs=3))
         results = ctx.enter_context(tc.tile_pool(name="results", bufs=8))
         kv_results = ctx.enter_context(tc.tile_pool(name="kv_results", bufs=2))
+        fm_results = ctx.enter_context(tc.tile_pool(name="fm_results", bufs=4))
         flipped = ctx.enter_context(tc.psum_pool(name="flipped", bufs=2))
         sums = ctx.enter_context(tc.psum_pool(name="sums", bufs=6))
         ctx.enter_context(tc.manual_schedule())
@@ -87,6 +91,19 @@ def tile_causalselfattentiongqa_pa_kernel(
         zeros = keep.tile([P, BANK], BF16)
         nc.vector.memset(zeros[:], 0.0)
         make_identity(nc, identity[:])
+        identity_bf = keep.tile([P, P], BF16)
+        swap = keep.tile([P, P], F32)
+        even = keep.tile([P, 1], F32)
+        sign = keep.tile([P, 1], F32)
+        doubled = keep.tile([P, BLOCKS, 2, HD], BF16)
+        fm_table = keep.tile([P, BLOCKS, 2, P], BF16)
+        id_pairs = identity[:].rearrange("p (i w) -> p i w", w=2)
+        swap_pairs = swap[:].rearrange("p (i w) -> p i w", w=2)
+        nc.gpsimd.tensor_copy(out=swap_pairs[:, :, 0:1], in_=id_pairs[:, :, 1:2])
+        nc.gpsimd.tensor_copy(out=swap_pairs[:, :, 1:2], in_=id_pairs[:, :, 0:1])
+        nc.scalar.copy(out=identity_bf[:], in_=identity[:])
+        nc.vector.tensor_reduce(out=even[:], in_=identity[:, 0:P:2], axis=mybir.AxisListType.X, op=ADD)
+        nc.vector.tensor_scalar(out=sign[:], in0=even[:], scalar1=2.0, scalar2=-1.0, op0=MULT, op1=ADD)
 
         def load_x(first_tile, count):
             tiles = slice(first_tile, first_tile + count)
@@ -337,6 +354,70 @@ def tile_causalselfattentiongqa_pa_kernel(
                 in_=parts[:, 0, some, :, :],
             )
 
+        def fm_doubled():
+            for s in range(BLOCKS):
+                nc.scalar.copy(
+                    out=doubled[:, s, :, :].rearrange("p c (i w) -> p c i w", w=2),
+                    in_=table_q[1][:, 1, HD * s : HD * (s + 1)]
+                    .rearrange("p (i c) -> p c i", c=2)
+                    .unsqueeze(3)
+                    .to_broadcast([P, 2, PAIRS, 2]),
+                )
+
+        def fm_tables():
+            table_t = flipped.tile([P, BLOCKS, 2, P], BF16, name="turned")
+            for s in range(BLOCKS):
+                for which in range(2):
+                    nc.tensor.transpose(table_t[:, s, which, :], doubled[:, s, which, :], identity_bf[:])
+            nc.scalar.copy(out=fm_table[:, :, 0, :], in_=table_t[:, :, 0, :])
+            nc.scalar.activation(
+                out=fm_table[:, :, 1, :], in_=table_t[:, :, 1, :], func=mybir.ActivationFunctionType.Copy, scale=sign[:, 0:1]
+            )
+
+        fm_accs = {}
+        fm_parts = {}
+
+        def project_fm(s, first_tile):
+            acc = sums.tile([P, BANK], F32, name="acc")
+            fm_accs[s] = acc
+            col = GROUP_COLS + HD * s - BANK
+            for place in range(QUAD):
+                r = first_tile + place
+                for c in range(PASSES):
+                    nc.tensor.matmul_mx(
+                        out=acc[:, P * place : P * (place + 1)],
+                        lhsT=w_rest[:, c, 2 * col : 2 * (col + HD)].bitcast(FP4X4),
+                        lhsT_scale=s_rest[:, c, col : col + HD],
+                        rhs=x_codes[:, r, P * c : P * (c + 1)].bitcast(FP8X4),
+                        rhs_scale=x_scales[:, r, P * c : P * (c + 1)],
+                        start=(c == 0),
+                        stop=(c == PASSES - 1),
+                    )
+
+        def products_fm(s):
+            parts = fm_results.tile([P, 2, QUAD, P], F32, name="fm_parts")
+            fm_parts[s] = parts
+            nc.vector.tensor_tensor(
+                out=parts[:],
+                in0=fm_accs[s][:].rearrange("f (r p) -> f r p", p=P).unsqueeze(1).to_broadcast([P, 2, QUAD, P]),
+                in1=fm_table[:, s, :, :].unsqueeze(2).to_broadcast([P, 2, QUAD, P]),
+                op=MULT,
+            )
+
+        def add_fm(s, first_tile):
+            parts = fm_parts[s]
+            total = flipped.tile([P, QUAD, HD], F32, name="turned")
+            for place in range(QUAD):
+                nc.tensor.matmul(
+                    out=total[:, place, :], lhsT=parts[:, 0, place, :], rhs=identity[:], start=True, stop=False, is_transpose=True
+                )
+                nc.tensor.matmul(
+                    out=total[:, place, :], lhsT=parts[:, 1, place, :], rhs=swap[:], start=False, stop=True, is_transpose=True
+                )
+            rows = fm_results.tile([P, QUAD, HD], F32, name="fm_rows")
+            nc.scalar.copy(out=rows[:], in_=total[:])
+            nc.sync.dma_start(out=q_rows[:, BLOCKS + s, first_tile : first_tile + QUAD, :], in_=rows[:])
+
         engines = {"g": nc.gpsimd, "v": nc.vector}
         for step in STEPS:
             op = step[0]
@@ -383,5 +464,15 @@ def tile_causalselfattentiongqa_pa_kernel(
                 waste = sums.tile([P, BANK], F32, name="acc")
                 for n in range(step[1]):
                     nc.tensor.matmul(out=waste[:], lhsT=zeros[:, 0:P], rhs=zeros[:], start=True, stop=True)
+            elif op == "FT":
+                fm_tables()
+            elif op == "FD":
+                fm_doubled()
+            elif op == "FM":
+                project_fm(step[1], step[2])
+            elif op == "FP":
+                products_fm(step[1])
+            elif op == "FA":
+                add_fm(step[1], step[2])
             elif op == "H":
                 nc.gpsimd.tensor_copy(out=seen[:], in_=x_codes[:, step[1], 0:1])

from contextlib import ExitStack

import concourse.mybir as mybir
from concourse.masks import make_identity

F32 = mybir.dt.float32
BF16 = mybir.dt.bfloat16
I32 = mybir.dt.int32
U32 = mybir.dt.uint32
U8 = mybir.dt.uint8
FP8X4 = mybir.dt.float8_e4m3fn_x4
FP4X4 = mybir.dt.float4_e2m1fn_x4
MULT = mybir.AluOpType.mult
ADD = mybir.AluOpType.add

P = 128
TOKENS = 1024
K = 1024
HD = 128
PAIRS = HD // 2
GROUPS = 2
Q_SLOTS = 4
GROUP_COLS = (Q_SLOTS + 2) * HD
COLS = GROUPS * GROUP_COLS
K_PASS = 4 * P
PASSES = K // K_PASS
TILES = TOKENS // P
BANK = 512
Q_BANKS = GROUPS * Q_SLOTS * HD // BANK
BLOCKS = BANK // HD
PAIR = 2

FLOPS = 2 * TOKENS * K * COLS


LOADS = [(1, 1), "SC0", "W0", "tq0", "w", "SC1", "tq1", (2, 2), "tk", (4, 2), (6, 2)]
STEPS = [
    ("D", 3), ("Sp", 0, 0), ("Zp", 0, 0), ("Sp", 0, 1), ("Zp", 0, 1), ("S", 1, 1), ("N", 0), ("M", 0, 0), ("Z", 1, 1), ("M", 1, 0), ("N", 1), ("FD",), ("M", 0, 1), ("M", 1, 1), ("S", 2, 2),
    ("P", 0, 0), ("P", 1, 0), ("A", 0, 0, "g"), ("P", 0, 1), ("P", 1, 1), ("Z", 2, 2), ("H", 2), ("A", 0, 1, "g"), ("N", 2), ("M", 0, 2), ("M", 1, 2), ("S", 4, 2),
    ("M", 2, 0), ("M", 3, 0), ("S", 6, 2), ("P", 0, 2), ("P", 1, 2),
    ("M", 2, 2), ("M", 3, 2), ("P", 2, 0), ("P", 3, 0), ("Z", 4, 2), ("Z", 6, 2), ("H", 6), ("A", 1, 0, "g"),
    ("M", 4, 0), ("M", 5, 0), ("FT",), ("P", 2, 2), ("P", 3, 2), ("A", 0, 2, "g"),
    ("M", 4, 2), ("M", 5, 2), ("P", 4, 0), ("P", 5, 0), ("A", 2, 0, "g"),
    ("FM", 0, 2), ("FM", 1, 2), ("P", 4, 2), ("P", 5, 2),
    ("M", 6, 2), ("M", 7, 2), ("FP", 0), ("FP", 1),
    ("FM", 2, 2), ("FM", 3, 2), ("FA", 0, 2), ("FA", 1, 2), ("P", 6, 2), ("P", 7, 2), ("A", 1, 2, "g"),
    ("M", 6, 0), ("M", 7, 0), ("FP", 2), ("FP", 3),
    ("M", 6, 1), ("M", 7, 1), ("FA", 2, 2), ("FA", 3, 2), ("P", 6, 0), ("P", 7, 0), ("Ah", 3, 0, 0, "g"),
    ("P", 6, 1), ("P", 7, 1), ("Ah", 3, 0, 1, "v"), ("Ah", 3, 1, 0, "v"), ("Ah", 3, 1, 1, "v"),
]


def tile_causalselfattentiongqa_pa_kernel(
    tc, x, freqs_cis, W_attn_words, W_attn_scales, out_0, out_1, out_2
):
    nc = tc.nc
    with ExitStack() as ctx:
        keep = ctx.enter_context(tc.tile_pool(name="keep", bufs=1))
        stage = ctx.enter_context(tc.tile_pool(name="stage", bufs=3))
        results = ctx.enter_context(tc.tile_pool(name="results", bufs=8))
        kv_results = ctx.enter_context(tc.tile_pool(name="kv_results", bufs=2))
        fm_results = ctx.enter_context(tc.tile_pool(name="fm_results", bufs=4))
        flipped = ctx.enter_context(tc.psum_pool(name="flipped", bufs=2))
        sums = ctx.enter_context(tc.psum_pool(name="sums", bufs=6))
        ctx.enter_context(tc.manual_schedule())

        x_view = x.rearrange("o (p r) k -> (o p) r k", r=TILES)
        q_rows = out_0.rearrange("o n h f -> (o n h) f").rearrange("(s p r) f -> p s r f", p=P, r=TILES)
        k_rows = out_1.rearrange("o n h f -> (o n h) f").rearrange("(g p r) f -> p g r f", p=P, r=TILES)
        v_rows = out_2.rearrange("o n h f -> (o n h) f").rearrange("(g p r) f -> p g r f", p=P, r=TILES)
        words_i32 = W_attn_words.bitcast(I32).rearrange("c p n -> p c n")
        scales_i32 = W_attn_scales.bitcast(I32)

        x_sb = keep.tile([P, TILES, K], BF16)
        x_codes = keep.tile([P, TILES, PASSES * P], U32, align_bytes=64)
        x_scales = keep.tile([P, TILES, PASSES * P], U8, align_bytes=64)
        w_first = keep.tile([P, PASSES, 2 * BANK], U8, align_bytes=64)
        w_rest = keep.tile([P, PASSES, 2 * (COLS - BANK)], U8, align_bytes=64)
        s_first = keep.tile([P, PASSES, BANK], U8, align_bytes=64)
        s_rest = keep.tile([P, PASSES, COLS - BANK], U8, align_bytes=64)
        table_q0 = keep.tile([P, 2, BANK], BF16)
        table_q1 = keep.tile([P, 2, BANK], BF16)
        table_q = [table_q0, table_q1]
        K_LEN = GROUPS * (TILES // 2) * HD
        table_k = keep.tile([P, 2 * K_LEN + 4], BF16)
        seen = keep.tile([P, 1], U32)
        identity = keep.tile([P, P], F32)

        nc.vector.memset(s_first[:].bitcast(I32), 0)
        nc.vector.memset(s_rest[:].bitcast(I32), 0)
        zeros = keep.tile([P, BANK], BF16)
        nc.vector.memset(zeros[:], 0.0)
        make_identity(nc, identity[:])
        identity_bf = keep.tile([P, P], BF16)
        swap = keep.tile([P, P], F32)
        even = keep.tile([P, 1], F32)
        sign = keep.tile([P, 1], F32)
        doubled = keep.tile([P, BLOCKS, 2, HD], BF16)
        fm_table = keep.tile([P, BLOCKS, 2, P], BF16)
        id_pairs = identity[:].rearrange("p (i w) -> p i w", w=2)
        swap_pairs = swap[:].rearrange("p (i w) -> p i w", w=2)
        nc.gpsimd.tensor_copy(out=swap_pairs[:, :, 0:1], in_=id_pairs[:, :, 1:2])
        nc.gpsimd.tensor_copy(out=swap_pairs[:, :, 1:2], in_=id_pairs[:, :, 0:1])
        nc.scalar.copy(out=identity_bf[:], in_=identity[:])
        nc.vector.tensor_reduce(out=even[:], in_=identity[:, 0:P:2], axis=mybir.AxisListType.X, op=ADD)
        nc.vector.tensor_scalar(out=sign[:], in0=even[:], scalar1=2.0, scalar2=-1.0, op0=MULT, op1=ADD)

        def load_x(first_tile, count):
            tiles = slice(first_tile, first_tile + count)
            nc.sync.dma_start(out=x_sb[:, tiles, :], in_=x_view[:, tiles, :])

        def load_words(tile, first_byte, n_bytes):
            nc.sync.dma_start(
                out=tile[:].bitcast(I32), in_=words_i32[:, :, first_byte // 4 : (first_byte + n_bytes) // 4]
            )

        q_bytes = 2 * Q_SLOTS * HD
        fc_q = freqs_cis.rearrange("(s p) i c -> p s (i c)", p=P)

        load_x(0, 1)

        def load_scales(tile, first_col, n_cols):
            for quadrant in range(4):
                nc.sync.dma_start(
                    out=tile[32 * quadrant : 32 * quadrant + 4, :, :].bitcast(I32),
                    in_=scales_i32[:, 4 * quadrant : 4 * quadrant + 4, first_col // 4 : (first_col + n_cols) // 4].rearrange(
                        "g r n -> r g n"
                    ),
                )

        def load_tq(bank):
            nc.sync.dma_start(
                out=table_q[bank][:, 1, :].rearrange("p (s f) -> p s f", f=HD),
                in_=fc_q[:, BLOCKS * bank : BLOCKS * (bank + 1), :],
            )

        def load_tk():
            nc.sync.dma_start(
                out=table_k[:, K_LEN + 2 : 2 * K_LEN + 2].rearrange("p (g n) -> p g n", g=GROUPS),
                in_=freqs_cis.rearrange("(g p j) i c -> p g (j i c)", g=GROUPS, p=P),
            )

        for what in LOADS:
            if what == "tq0":
                load_tq(0)
            elif what == "tq1":
                load_tq(1)
            elif what == "W0":
                load_words(w_first, 0, q_bytes)
            elif what == "SC0":
                load_scales(s_first, 0, BANK)
            elif what == "SC1":
                load_scales(s_rest, BANK, COLS - BANK)
            elif what == "tk":
                load_tk()
            elif what == "w":
                load_words(w_rest, q_bytes, 2 * COLS - q_bytes)
            else:
                load_x(what[0], what[1])

        def negate(bank):
            nc.scalar.mul(out=table_q[bank][:, 0, :], in_=table_q[bank][:, 1, :], mul=-1.0)

        def turned_q(bank):
            shifted = (
                table_q[bank][:].rearrange("p w l -> p (w l)")[:, 1 : 2 * BANK - 1].rearrange("p (two j) -> p two j", two=2)
            )
            return shifted[:, :, 0 : BANK - 1 : 2].rearrange("p two (s i) -> p s i two", i=PAIRS)

        def negate_k():
            nc.scalar.mul(out=table_k[:, 0:K_LEN], in_=table_k[:, K_LEN + 2 : 2 * K_LEN + 2], mul=-1.0)

        cd_k = table_k[:, K_LEN + 2 : 2 * K_LEN + 2].rearrange("p (g j i two) -> p j g i two", g=GROUPS, i=PAIRS, two=2)
        dc_k = (
            table_k[:, 1 : 2 * K_LEN + 3]
            .rearrange("p (two n) -> p two n", two=2)[:, :, 0:K_LEN]
            .rearrange("p two (g j i e) -> p e j g i two", g=GROUPS, i=PAIRS, e=2)[:, 0]
        )

        staged = {}

        def stage_tiles(first_tile, count):
            grouped = stage.tile([P, count, PASSES * P * 4], BF16, align_bytes=64, name="grouped")
            staged[first_tile] = grouped
            for n in range(count):
                x_words = x_sb[:, first_tile + n, :].bitcast(F32)
                turned = flipped.tile([P, PASSES, 2, P], F32, name="turned")
                for c in range(PASSES):
                    for u in range(2):
                        nc.tensor.transpose(
                            turned[:, c, u, :], x_words[:, K_PASS // 2 * c + u : K_PASS // 2 * (c + 1) : 2], identity[:]
                        )
                nc.scalar.copy(
                    out=grouped[:, n, :].bitcast(F32).rearrange("p (c t u) -> p c t u", c=PASSES, u=2),
                    in_=turned[:].rearrange("p c u t -> p c t u"),
                )

        whole = {}

        def stage_pass(r, c):
            if r not in staged:
                first = stage.tile([P, 1, PASSES * P * 4], BF16, align_bytes=64, name="grouped")
                staged[r] = first
                x_words = x_sb[:, r, :].bitcast(F32)
                turned = flipped.tile([P, PASSES, 2, P], F32, name="turned")
                whole[r] = turned
                for cc in range(PASSES):
                    for u in range(2):
                        nc.tensor.transpose(
                            turned[:, cc, u, :], x_words[:, K_PASS // 2 * cc + u : K_PASS // 2 * (cc + 1) : 2], identity[:]
                        )
            nc.scalar.copy(
                out=staged[r][:, 0, K_PASS * c : K_PASS * (c + 1)].bitcast(F32).rearrange("p (t u) -> p t u", u=2),
                in_=whole[r][:, c, :, :].rearrange("p u t -> p t u"),
            )

        def quantise_pass(r, c):
            nc.vector.quantize_mx(
                out=x_codes[:, r, P * c : P * (c + 1)].bitcast(FP8X4),
                scales=x_scales[:, r, P * c : P * (c + 1)],
                in_=staged[r][:, 0, K_PASS * c : K_PASS * (c + 1)],
            )

        def quantise(first_tile, count):
            tiles = slice(first_tile, first_tile + count)
            nc.vector.quantize_mx(
                out=x_codes[:, tiles, :].rearrange("p r w -> p (r w)").bitcast(FP8X4),
                scales=x_scales[:, tiles, :].rearrange("p r w -> p (r w)"),
                in_=staged[first_tile][:].rearrange("p r w -> p (r w)"),
            )

        def multiply(acc, r, first_col, n_cols):
            words, scale_bytes, shift = (w_first, s_first, 0) if first_col < BANK else (w_rest, s_rest, BANK)
            for c in range(PASSES):
                nc.tensor.matmul_mx(
                    out=acc,
                    lhsT=x_codes[:, r, P * c : P * (c + 1)].bitcast(FP8X4),
                    lhsT_scale=x_scales[:, r, P * c : P * (c + 1)],
                    rhs=words[:, c, 2 * (first_col - shift) : 2 * (first_col - shift + n_cols)].bitcast(FP4X4),
                    rhs_scale=scale_bytes[:, c, first_col - shift : first_col - shift + n_cols],
                    start=(c == 0),
                    stop=(c == PASSES - 1),
                )

        accs = {}

        def project(r, bank):
            acc = sums.tile([P, BANK], F32, name="acc")
            accs[(r, bank)] = acc
            if bank < Q_BANKS:
                multiply(acc[:], r, GROUP_COLS * bank, BANK)
            else:
                for g in range(GROUPS):
                    for slot in range(2):
                        multiply(
                            acc[:, HD * (GROUPS * slot + g) : HD * (GROUPS * slot + g + 1)],
                            r,
                            GROUP_COLS * g + HD * (Q_SLOTS + slot),
                            HD,
                        )

        q_parts = {}

        def product(r, bank, which):
            pair, place = r // PAIR, r % PAIR
            if (pair, bank) not in q_parts:
                new_parts = results.tile([P, 2, BLOCKS, PAIR, HD], F32, name="q_parts")
                q_parts[(pair, bank)] = new_parts
            parts = q_parts[(pair, bank)]
            u = accs[(r, bank)][:].rearrange("p (s i w) -> p w s i", i=PAIRS, w=2)
            if which == 0:
                table = table_q[bank][:, 1, :].rearrange("p (s i two) -> p s i two", i=PAIRS, two=2)
            else:
                table = turned_q(bank)
            nc.vector.tensor_tensor(
                out=parts[:, which, :, place, :].rearrange("p s (i two) -> p s i two", two=2),
                in0=u[:, which, :, :].unsqueeze(3).to_broadcast([P, BLOCKS, PAIRS, 2]),
                in1=table,
                op=MULT,
            )

        def both(r, bank):
            product(r, bank, 0)
            product(r, bank, 1)

        def add_up(parts, engine):
            flat_a = parts[:, 0, :, :, :].rearrange("p s t f -> p (s t f)")
            engine.tensor_tensor(
                out=flat_a, in0=flat_a, in1=parts[:, 1, :, :, :].rearrange("p s t f -> p (s t f)"), op=ADD
            )

        def finish(pair, bank, engine):
            parts = q_parts[(pair, bank)]
            blocks = slice(BLOCKS * bank, BLOCKS * (bank + 1))
            add_up(parts, engine)
            nc.sync.dma_start(out=q_rows[:, blocks, PAIR * pair : PAIR * (pair + 1), :], in_=parts[:, 0, :, :, :])

        QUAD = 4

        k_parts = {}
        v_parts = {}

        def keys(r):
            quad, place = r // QUAD, r % QUAD
            if quad not in k_parts:
                new_k = kv_results.tile([P, 2, GROUPS, QUAD, HD], F32, name="k_parts")
                new_v = kv_results.tile([P, GROUPS, QUAD, HD], F32, name="v")
                k_parts[quad] = new_k
                v_parts[quad] = new_v
            acc = accs[(r, Q_BANKS)]
            u = acc[:, 0 : GROUPS * HD].rearrange("p (s i w) -> p w s i", i=PAIRS, w=2)
            for which in range(2):
                nc.vector.tensor_tensor(
                    out=k_parts[quad][:, which, :, place, :].rearrange("p s (i two) -> p s i two", two=2),
                    in0=u[:, which, :, :].unsqueeze(3).to_broadcast([P, GROUPS, PAIRS, 2]),
                    in1=(cd_k if which == 0 else dc_k)[:, r // 2],
                    op=MULT,
                )
            nc.scalar.copy(
                out=v_parts[quad][:, :, place, :], in_=acc[:, GROUPS * HD : BANK].rearrange("p (g f) -> p g f", f=HD)
            )
            if place == QUAD - 1:
                nc.sync.dma_start(out=v_rows[:, :, QUAD * quad : QUAD * (quad + 1), :], in_=v_parts[quad][:])

        def finish_k(quad, engine):
            add_up(k_parts[quad], engine)
            nc.sync.dma_start(out=k_rows[:, :, QUAD * quad : QUAD * (quad + 1), :], in_=k_parts[quad][:, 0, :, :, :])

        def add_k_pair(pair, engine):
            parts = k_parts[pair // 2]
            places = slice(PAIR * (pair % 2), PAIR * (pair % 2) + PAIR)
            engine.tensor_tensor(
                out=parts[:, 0, :, places, :].rearrange("p g t f -> p g (t f)"),
                in0=parts[:, 0, :, places, :].rearrange("p g t f -> p g (t f)"),
                in1=parts[:, 1, :, places, :].rearrange("p g t f -> p g (t f)"),
                op=ADD,
            )
            if pair % 2 == 1:
                quad = pair // 2
                nc.sync.dma_start(out=k_rows[:, :, QUAD * quad : QUAD * (quad + 1), :], in_=parts[:, 0, :, :, :])

        def finish_half(pair, bank, half, engine):
            parts = q_parts[(pair, bank)]
            some = slice(BLOCKS // 2 * half, BLOCKS // 2 * (half + 1))
            engine.tensor_tensor(
                out=parts[:, 0, some, :, :].rearrange("p s t f -> p (s t f)"),
                in0=parts[:, 0, some, :, :].rearrange("p s t f -> p (s t f)"),
                in1=parts[:, 1, some, :, :].rearrange("p s t f -> p (s t f)"),
                op=ADD,
            )
            first_block = BLOCKS * bank + BLOCKS // 2 * half
            nc.sync.dma_start(
                out=q_rows[:, first_block : first_block + BLOCKS // 2, PAIR * pair : PAIR * (pair + 1), :],
                in_=parts[:, 0, some, :, :],
            )

        def fm_doubled():
            for s in range(BLOCKS):
                nc.scalar.copy(
                    out=doubled[:, s, :, :].rearrange("p c (i w) -> p c i w", w=2),
                    in_=table_q[1][:, 1, HD * s : HD * (s + 1)]
                    .rearrange("p (i c) -> p c i", c=2)
                    .unsqueeze(3)
                    .to_broadcast([P, 2, PAIRS, 2]),
                )

        def fm_tables():
            table_t = flipped.tile([P, BLOCKS, 2, P], BF16, name="turned")
            for s in range(BLOCKS):
                for which in range(2):
                    nc.tensor.transpose(table_t[:, s, which, :], doubled[:, s, which, :], identity_bf[:])
            nc.scalar.copy(out=fm_table[:, :, 0, :], in_=table_t[:, :, 0, :])
            nc.scalar.activation(
                out=fm_table[:, :, 1, :], in_=table_t[:, :, 1, :], func=mybir.ActivationFunctionType.Copy, scale=sign[:, 0:1]
            )

        fm_accs = {}
        fm_parts = {}

        def project_fm(s, first_tile):
            acc = sums.tile([P, BANK], F32, name="acc")
            fm_accs[s] = acc
            col = GROUP_COLS + HD * s - BANK
            for place in range(QUAD):
                r = first_tile + place
                for c in range(PASSES):
                    nc.tensor.matmul_mx(
                        out=acc[:, P * place : P * (place + 1)],
                        lhsT=w_rest[:, c, 2 * col : 2 * (col + HD)].bitcast(FP4X4),
                        lhsT_scale=s_rest[:, c, col : col + HD],
                        rhs=x_codes[:, r, P * c : P * (c + 1)].bitcast(FP8X4),
                        rhs_scale=x_scales[:, r, P * c : P * (c + 1)],
                        start=(c == 0),
                        stop=(c == PASSES - 1),
                    )

        def products_fm(s):
            parts = fm_results.tile([P, 2, QUAD, P], F32, name="fm_parts")
            fm_parts[s] = parts
            nc.vector.tensor_tensor(
                out=parts[:],
                in0=fm_accs[s][:].rearrange("f (r p) -> f r p", p=P).unsqueeze(1).to_broadcast([P, 2, QUAD, P]),
                in1=fm_table[:, s, :, :].unsqueeze(2).to_broadcast([P, 2, QUAD, P]),
                op=MULT,
            )

        def add_fm(s, first_tile):
            parts = fm_parts[s]
            total = flipped.tile([P, QUAD, HD], F32, name="turned")
            for place in range(QUAD):
                nc.tensor.matmul(
                    out=total[:, place, :], lhsT=parts[:, 0, place, :], rhs=identity[:], start=True, stop=False, is_transpose=True
                )
                nc.tensor.matmul(
                    out=total[:, place, :], lhsT=parts[:, 1, place, :], rhs=swap[:], start=False, stop=True, is_transpose=True
                )
            rows = fm_results.tile([P, QUAD, HD], F32, name="fm_rows")
            nc.scalar.copy(out=rows[:], in_=total[:])
            nc.sync.dma_start(out=q_rows[:, BLOCKS + s, first_tile : first_tile + QUAD, :], in_=rows[:])

        engines = {"g": nc.gpsimd, "v": nc.vector}
        for step in STEPS:
            op = step[0]
            if op == "S":
                stage_tiles(step[1], step[2])
            elif op == "Z":
                quantise(step[1], step[2])
            elif op == "N":
                if step[1] == 2:
                    negate_k()
                else:
                    negate(step[1])
            elif op == "M":
                project(step[1], step[2])
            elif op == "P":
                if step[2] == 2:
                    keys(step[1])
                else:
                    both(step[1], step[2])
            elif op == "A":
                if step[2] == 2:
                    finish_k(step[1], engines[step[3]])
                else:
                    finish(step[1], step[2], engines[step[3]])
            elif op == "a":
                r, bank = step[1], step[2]
                parts = q_parts[(r // PAIR, bank)]
                nc.vector.tensor_tensor(
                    out=parts[:, 0, :, r % PAIR, :], in0=parts[:, 0, :, r % PAIR, :], in1=parts[:, 1, :, r % PAIR, :], op=ADD
                )
                if r % PAIR == PAIR - 1:
                    nc.sync.dma_start(
                        out=q_rows[:, BLOCKS * bank : BLOCKS * (bank + 1), r - 1 : r + 1, :], in_=parts[:, 0, :, :, :]
                    )
            elif op == "Sp":
                stage_pass(step[1], step[2])
            elif op == "Zp":
                quantise_pass(step[1], step[2])
            elif op == "Ak":
                add_k_pair(step[1], engines[step[2]])
            elif op == "Ah":
                finish_half(step[1], step[2], step[3], engines[step[4]])
            elif op == "D":
                waste = sums.tile([P, BANK], F32, name="acc")
                for n in range(step[1]):
                    nc.tensor.matmul(out=waste[:], lhsT=zeros[:, 0:P], rhs=zeros[:], start=True, stop=True)
            elif op == "FT":
                fm_tables()
            elif op == "FD":
                fm_doubled()
            elif op == "FM":
                project_fm(step[1], step[2])
            elif op == "FP":
                products_fm(step[1])
            elif op == "FA":
                add_fm(step[1], step[2])
            elif op == "H":
                nc.gpsimd.tensor_copy(out=seen[:], in_=x_codes[:, step[1], 0:1])
